import numpy as np
import ml_dtypes


def mxq(x, axis, fmt="e4m3"):
    dtype, down = {"e4m3": (ml_dtypes.float8_e4m3fn, 7), "e5m2": (ml_dtypes.float8_e5m2, 14)}[fmt]
    v = np.moveaxis(np.asarray(x, np.float32).astype(ml_dtypes.bfloat16).astype(np.float64), axis, -1)
    blocks = v.reshape(v.shape[:-1] + (-1, 32))
    amax = np.abs(blocks).max(-1, keepdims=True)
    byte = np.maximum(np.where(amax > 0, np.frexp(amax)[1] - 1 + 127, 0) - down, 1)
    scale = np.exp2(byte - 127.0)
    codes = (blocks / scale).astype(np.float32).astype(dtype).astype(np.float64)
    return np.moveaxis((codes * scale).reshape(v.shape), -1, axis)


WIDE = False


def mx_kscale(k):
    if not WIDE:
        return np.ones(k)
    levels = np.array([10, -10, 5, -5, 0])
    if k % 512:
        return np.exp2(np.random.permutation(np.resize(levels, k // 32))).repeat(32)
    a = np.empty((k // 512, 16))
    for p in range(k // 512):
        a[p, :8] = np.random.permutation(np.resize(levels, 8))
        for g in range(8):
            far = levels[np.abs(levels - a[p, g]) >= 10]
            a[p, g + 8] = far[np.random.randint(len(far))]
    return np.exp2(a.ravel()).repeat(32)


BF16 = ml_dtypes.bfloat16


def bf(x):
    return np.asarray(x, np.float32).astype(BF16)


def f64(x):
    return np.asarray(x).astype(np.float64)


B, N, D, H, HD, S, DO = 2, 4096, 1024, 2, 64, 11, 1024
E = H * HD
D4 = [0.4829629131445341, 0.8365163037378079, 0.2241438680420134, -0.1294095225512604]
T = len(D4)


def elu1(u):
    return np.where(u > 0.0, u, np.exp(np.minimum(u, 0.0)) - 1.0) + 1.0


def softplus(u):
    return np.log(1.0 + np.exp(u))


def shifted(t, o):
    if o == 0:
        return t
    return np.concatenate([np.zeros((B, H, o, HD)), t[:, :, :N - o, :]], axis=2)


def setup_inputs():
    s = mx_kscale(D)
    lg = np.random.standard_normal((B, H, N, S)) * 1.4
    g = np.exp(lg - lg.max(-1, keepdims=True))
    return {"x": bf(np.random.standard_normal((B, N, D)) * s),
            "W_qkv": bf(np.random.standard_normal((3 * E, D)) * 0.6 / np.sqrt(D) / s),
            "b_qkv": bf(np.random.standard_normal(3 * E) * 0.1),
            "gains": bf(g / g.sum(-1, keepdims=True)),
            "pos_bias": bf(np.random.standard_normal((S * T, H)) * 0.5),
            "identity_bypass": bf(-1.0 + 0.5 * np.random.standard_normal(H))}


def reference(x, W_qkv, b_qkv, gains, pos_bias, identity_bypass):
    qkv = (mxq(f64(x), 2, "e4m3") @ mxq(f64(W_qkv), 1, "e4m3").T) + f64(b_qkv)
    q, k, v = [t.reshape(B, N, H, HD).transpose(0, 2, 1, 3) for t in np.split(qkv, 3, axis=-1)]
    g, pb = f64(gains), f64(pos_bias)
    acc = np.zeros((B, H, N, HD))
    z = np.zeros((B, H, N, 1))
    tap = 0
    for j in range(S):
        d = 1 << j
        g_j = g[..., j][..., None]
        for tau, c in enumerate(D4):
            o = d * tau
            bias = pb[tap].reshape(1, H, 1, 1)
            tap += 1
            if o != 0 and o >= N:
                continue
            k_s, v_s = shifted(k, o), shifted(v, o)
            feat = elu1(np.sum(q * k_s, -1, keepdims=True) + bias)
            acc = acc + (g_j * c) * feat * v_s
            z = z + g_j * abs(c) * feat
    p = softplus(f64(identity_bypass)).reshape(1, H, 1, 1)
    local = elu1(np.sum(q * k, -1, keepdims=True))
    acc = acc + p * local * v
    z = z + p * local
    res = acc / (z + 1e-06)
    return res.transpose(0, 2, 1, 3).reshape(B, N, E)

@@ -1,0 +1,410 @@
+from contextlib import ExitStack
+
+import concourse.mybir as mybir
+from concourse.masks import make_identity
+
+F32 = mybir.dt.float32
+BF16 = mybir.dt.bfloat16
+U32 = mybir.dt.uint32
+U8 = mybir.dt.uint8
+FP8X4 = mybir.dt.float8_e4m3fn_x4
+ALU = mybir.AluOpType
+ACTF = mybir.ActivationFunctionType
+AX = mybir.AxisListType
+
+P = 128
+B, N, D, H, HD, NS = 2, 4096, 1024, 2, 64, 11
+E = H * HD
+CH = 512
+TPC = CH // P
+NCC = N // CH
+NT = N // P
+NCHUNK = B * NCC
+D4 = (0.4829629131445341, 0.8365163037378079, 0.2241438680420134, -0.1294095225512604)
+OFFS = tuple(sorted([0] + [1 << i for i in range(12)] + [3 << j for j in range(11)]))
+NOFF = len(OFFS)
+NTAP = 1 + 4 * NS
+NEAR = 15
+NFEW = 6
+KWIN = 256
+VWIN = 64
+ROW = 2 * P + 1
+UNIT = P * ROW
+VRING = 48
+BRING = 16
+SCR0 = B * N * E - H * TPC * UNIT
+HOLD0 = SCR0 // (CH * E)
+FLOPS = 2 * B * N * D * 3 * E + 4 * B * H * N * HD * NOFF
+
+
+def n_valid(t):
+    return len([o for o in OFFS if o <= t * P + P - 1])
+
+
+def cut_groups(nv):
+    cut = [s for s in range(nv) if OFFS[s] % P != 0]
+    return [cut[i:i + 4] for i in range(0, len(cut), 4)]
+
+
+def runs_of(places):
+    runs = []
+    for i, s in enumerate(places):
+        if runs and runs[-1][1] + runs[-1][2] == s:
+            runs[-1][2] += 1
+        else:
+            runs.append([i, s, 1])
+    return runs
+
+
+def tile_dwarfattention_pa_t_kernel(tc, x, W_qkv, b_qkv, gains, pos_bias, identity_bypass, out):
+    nc = tc.nc
+    with ExitStack() as ctx:
+        const = ctx.enter_context(tc.tile_pool(name="const", bufs=1))
+        ps_tr = ctx.enter_context(tc.psum_pool(name="ps_tr", bufs=2))
+        ps_mx = ctx.enter_context(tc.psum_pool(name="ps_mx", bufs=1))
+        ps_cut = ctx.enter_context(tc.psum_pool(name="ps_cut", bufs=4))
+        ps_near = ctx.enter_context(tc.psum_pool(name="ps_near", bufs=1))
+
+        ident = const.tile([P, P], F32, name="ident")
+        make_identity(nc, ident[:])
+        w_codes = const.tile([P, 2, 3 * P], U32, name="w_codes", align_bytes=64)
+        w_scales = const.tile([P, 2, 3 * P], U8, name="w_scales", align_bytes=64)
+        bias_col = const.tile([P, 4], F32, name="bias_col")
+        pb_bc = const.tile([P, H, NTAP], F32, name="pb_bc")
+        g_raw = const.tile([P, B, H, NT, NS], BF16, name="g_raw")
+        bypass = const.tile([P, H], F32, name="bypass")
+        k_tok = const.tile([P, NT, E], F32, name="k_tok")
+        v_tok = const.tile([P, VRING, E], F32, name="v_tok")
+        v_half = const.tile([P, BRING, E], F32, name="v_half")
+        held = const.tile([P, (NCHUNK - HOLD0) * TPC, E], F32, name="held")
+        spare = const.tile([P, HD], F32, name="spare")
+        rows = const.tile([P, H, TPC, ROW], F32, name="rows")
+        nc.gpsimd.memset(rows[:], 0.0)
+
+        with tc.tile_pool(name="setup", bufs=1) as setup:
+            w_sb = setup.tile([P, 3, D], BF16, name="w_sb")
+            nc.sync.dma_start(out=w_sb[:], in_=W_qkv.rearrange("(f p) k -> p f k", p=P))
+            b_rows = setup.tile([P, P], BF16, name="b_rows")
+            nc.vector.memset(b_rows[:], 0.0)
+            nc.scalar.dma_start(out=b_rows[0:3, :], in_=b_qkv.rearrange("(f c) -> f c", c=P))
+            pb_raw = setup.tile([P, 4 * NS * H], BF16, name="pb_raw")
+            nc.scalar.dma_start(out=pb_raw[:], in_=pos_bias.rearrange("r h -> (r h)").partition_broadcast(P))
+            ib_raw = setup.tile([P, H], BF16, name="ib_raw")
+            nc.scalar.dma_start(out=ib_raw[:], in_=identity_bypass.partition_broadcast(P))
+            for b in range(B):
+                for h in range(H):
+                    nc.scalar.dma_start(out=g_raw[:, b, h, :, :], in_=gains[b, h].rearrange("(t p) j -> p t j", p=P))
+
+            w_grouped = setup.tile([P, 2, 3 * P, 2], F32, name="w_grouped", align_bytes=64)
+            for f in range(3):
+                w_tr = ps_tr.tile([P, 4, P], F32, name="w_tr", tag="tr")
+                words = w_sb[:, f, :].bitcast(F32)
+                for g in range(2):
+                    for u in range(2):
+                        nc.tensor.transpose(out=w_tr[:, 2 * g + u, :],
+                                            in_=words[:, 2 * P * g + u:2 * P * (g + 1):2], identity=ident[:])
+                nc.vector.tensor_copy(out=w_grouped[:, :, f * P:(f + 1) * P, :],
+                                      in_=w_tr[:].rearrange("p (g u) r -> p g r u", u=2))
+            for g in range(2):
+                for f in range(3):
+                    nc.vector.quantize_mx(
+                        out=w_codes[:, g, f * P:(f + 1) * P].bitcast(FP8X4),
+                        scales=w_scales[:, g, f * P:(f + 1) * P],
+                        in_=w_grouped[:, g, f * P:(f + 1) * P, :].rearrange("p r u -> p (r u)").bitcast(BF16))
+
+            b_rows32 = setup.tile([P, P], F32, name="b_rows32")
+            nc.vector.tensor_copy(out=b_rows32[:], in_=b_rows[:])
+            b_tr = ps_tr.tile([P, 4, P], F32, name="b_tr", tag="tr")
+            nc.tensor.transpose(out=b_tr[:, 0, :], in_=b_rows32[:], identity=ident[:])
+            nc.vector.tensor_copy(out=bias_col[:, 0:3], in_=b_tr[:, 0, 0:3])
+
+            nc.vector.memset(pb_bc[:], 0.0)
+            nc.vector.tensor_copy(out=pb_bc[:, :, 1:NTAP].rearrange("p h (t j) -> p h t j", t=4),
+                                  in_=pb_raw[:].rearrange("p (j t h) -> p h t j", t=4, h=H))
+
+            ib = setup.tile([P, H], F32, name="ib")
+            nc.vector.tensor_copy(out=ib[:], in_=ib_raw[:])
+            ib_e = setup.tile([P, H], F32, name="ib_e")
+            nc.scalar.activation(out=ib_e[:], in_=ib[:], func=ACTF.Abs)
+            nc.scalar.activation(out=ib_e[:], in_=ib_e[:], func=ACTF.Exp, scale=-1.0)
+            nc.vector.tensor_scalar_add(out=ib_e[:], in0=ib_e[:], scalar1=1.0)
+            nc.scalar.activation(out=ib_e[:], in_=ib_e[:], func=ACTF.Ln)
+            nc.vector.scalar_tensor_tensor(out=bypass[:], in0=ib[:], scalar=0.0, in1=ib_e[:],
+                                           op0=ALU.max, op1=ALU.add)
+
+        x_pool = ctx.enter_context(tc.tile_pool(name="x_pool", bufs=2))
+        grouped_pool = ctx.enter_context(tc.tile_pool(name="grouped_pool", bufs=2))
+        code_pool = ctx.enter_context(tc.tile_pool(name="code_pool", bufs=2))
+        kf_pool = ctx.enter_context(tc.tile_pool(name="kf_pool", bufs=3))
+        vf_pool = ctx.enter_context(tc.tile_pool(name="vf_pool", bufs=3))
+        q_pool = ctx.enter_context(tc.tile_pool(name="q_pool", bufs=3))
+        prod_pool = ctx.enter_context(tc.tile_pool(name="prod_pool", bufs=3))
+        score_pool = ctx.enter_context(tc.tile_pool(name="score_pool", bufs=3))
+        tap_pool = ctx.enter_context(tc.tile_pool(name="tap_pool", bufs=3))
+        band_pool = ctx.enter_context(tc.tile_pool(name="band_pool", bufs=2))
+        out_pool = ctx.enter_context(tc.tile_pool(name="out_pool", bufs=2))
+
+        x_of, grouped_of, code_of = {}, {}, {}
+        kf_of, vf_of, q_of = {}, {}, {}
+        score_of, weight_of, skewed_of, band_of, o_of = {}, {}, {}, {}, {}
+        scratch = out.rearrange("b n e -> (b n e)")
+
+        def feature_major(c):
+            if c not in kf_of:
+                kf_of[c] = kf_pool.tile([P, KWIN + CH], F32, name="kf")
+                vf_of[c] = vf_pool.tile([P, VWIN + CH], F32, name="vf")
+            return kf_of[c], vf_of[c]
+
+        def load_x(c):
+            b, cc = divmod(c, NCC)
+            x_of[c] = x_pool.tile([P, TPC, D], BF16, name="x_sb")
+            nc.sync.dma_start(out=x_of[c][:],
+                              in_=x[b, cc * CH:(cc + 1) * CH, :].rearrange("(t p) k -> p t k", p=P))
+
+        def transpose_x(c, tl):
+            if tl == 0:
+                grouped_of[c] = grouped_pool.tile([P, 2, CH, 2], F32, name="grouped", align_bytes=64)
+            x_tr = ps_tr.tile([P, 4, P], F32, name="x_tr", tag="tr")
+            words = x_of[c][:, tl, :].bitcast(F32)
+            for g in range(2):
+                for u in range(2):
+                    nc.tensor.transpose(out=x_tr[:, 2 * g + u, :],
+                                        in_=words[:, 2 * P * g + u:2 * P * (g + 1):2], identity=ident[:])
+            nc.scalar.copy(out=grouped_of[c][:, :, tl * P:(tl + 1) * P, :],
+                           in_=x_tr[:].rearrange("p (g u) r -> p g r u", u=2))
+
+        def quantise_x(c):
+            codes = code_pool.tile([P, 2, CH], U32, name="codes", align_bytes=64)
+            scales = code_pool.tile([P, 2, CH], U8, name="scales", align_bytes=64)
+            for g in range(2):
+                nc.vector.quantize_mx(
+                    out=codes[:, g, :].bitcast(FP8X4), scales=scales[:, g, :],
+                    in_=grouped_of[c][:, g, :, :].rearrange("p r u -> p (r u)").bitcast(BF16))
+            code_of[c] = (codes, scales)
+
+        def project(c, f):
+            codes, scales = code_of[c]
+            acc = ps_mx.tile([P, CH], F32, name="acc", tag="mx")
+            for g in range(2):
+                nc.tensor.matmul_mx(out=acc[:], lhsT=w_codes[:, g, f * P:(f + 1) * P].bitcast(FP8X4),
+                                    lhsT_scale=w_scales[:, g, f * P:(f + 1) * P],
+                                    rhs=codes[:, g, :].bitcast(FP8X4), rhs_scale=scales[:, g, :],
+                                    start=(g == 0), stop=(g == 1))
+            return acc
+
+        def add_bias(dst, acc, f):
+            nc.scalar.activation(out=dst, in_=acc, func=ACTF.Identity, bias=bias_col[:, f:f + 1], scale=1.0)
+
+        def project_kv(c):
+            cc = c % NCC
+            for f, win in ((1, KWIN), (2, VWIN)):
+                dst = feature_major(c)[f - 1]
+                if cc == 0:
+                    nc.vector.memset(dst[:, 0:win], 0.0)
+                acc = project(c, f)
+                add_bias(dst[:, win:win + CH], acc[:], f)
+                if cc + 1 < NCC:
+                    add_bias(feature_major(c + 1)[f - 1][:, 0:win], acc[:, CH - win:CH], f)
+
+        def token_major(src, first, dst):
+            tr = ps_tr.tile([P, TPC, P], F32, name="tok_tr", tag="tr")
+            for tl in range(TPC):
+                nc.tensor.transpose(out=tr[:, tl, :], in_=src[:, first + tl * P:first + (tl + 1) * P],
+                                    identity=ident[:])
+            nc.scalar.copy(out=dst, in_=tr[:])
+
+        def project_q(c):
+            q_f = q_pool.tile([P, CH], F32, name="q_f")
+            add_bias(q_f[:], project(c, 0)[:], 0)
+            q_of[c] = q_pool.tile([P, TPC, E], F32, name="q_tok")
+            token_major(q_f, 0, q_of[c][:])
+
+        def turn_kv(c):
+            cc = c % NCC
+            g0 = c * TPC
+            token_major(kf_of[c], KWIN, k_tok[:, cc * TPC:(cc + 1) * TPC, :])
+            token_major(vf_of[c], VWIN, v_tok[:, g0 % VRING:g0 % VRING + TPC, :])
+            token_major(vf_of[c], 0, v_half[:, g0 % BRING:g0 % BRING + TPC, :])
+
+        def scores(c, tl):
+            cc = c % NCC
+            if tl == 0:
+                s_all = score_pool.tile([P, H, TPC, NOFF], F32, name="s_all")
+                s_few = score_pool.tile([P, H, TPC, NFEW], F32, name="s_few")
+                score_of[c] = (s_all, s_few)
+                if n_valid(cc * TPC) < NOFF:
+                    nc.vector.memset(s_all[:], 0.0)
+            s_all, s_few = score_of[c]
+            t = cc * TPC + tl
+            nv = n_valid(t)
+            q_t = q_of[c][:, tl, :]
+            prod = prod_pool.tile([P, NOFF, E], F32, name="prod")
+            for places in cut_groups(nv):
+                cut = ps_cut.tile([P, 4, P], F32, name="cut", tag="cut")
+                for i, s in enumerate(places):
+                    first = KWIN + tl * P - OFFS[s]
+                    nc.tensor.transpose(out=cut[:, i, :], in_=kf_of[c][:, first:first + P], identity=ident[:])
+                for i0, s0, ln in runs_of(places):
+                    nc.vector.tensor_tensor(out=prod[:, s0:s0 + ln, :], in0=cut[:, i0:i0 + ln, :],
+                                            in1=q_t.unsqueeze(1).to_broadcast([P, ln, E]), op=ALU.mult)
+            for s in range(nv):
+                if OFFS[s] % P == 0:
+                    nc.vector.tensor_tensor(out=prod[:, s, :], in0=k_tok[:, t - OFFS[s] // P, :], in1=q_t,
+                                            op=ALU.mult)
+            for s in range(NFEW):
+                for h in range(H):
+                    nc.scalar.activation(out=spare[:], in_=prod[:, s, h * HD:(h + 1) * HD], func=ACTF.Copy,
+                                         accum_out=s_few[:, h, tl, s:s + 1])
+            nc.vector.tensor_reduce(out=s_all[:, :, tl, NFEW:nv].rearrange("p h s -> p s h"),
+                                    in_=prod[:, NFEW:nv, :].rearrange("p s (h d) -> p s h d", h=H),
+                                    axis=AX.X, op=ALU.add)
+
+        def weights(c):
+            b, cc = divmod(c, NCC)
+            s_all, s_few = score_of[c]
+            shape = [P, H, TPC, NTAP]
+            nf = (NFEW - 2) // 2
+            few = s_few[:, :, :, 2:NFEW].rearrange("p h t (i two) -> p h t i two", two=2)
+            pairs = s_all[:, :, :, NFEW:NOFF].rearrange("p h t (i two) -> p h t i two", two=2)
+            u = tap_pool.tile(shape, F32, name="u")
+            nc.scalar.copy(out=u[:, :, :, 0:12], in_=s_few[:, :, :, 0:1].to_broadcast([P, H, TPC, 12]))
+            nc.scalar.copy(out=u[:, :, :, 12:13], in_=s_few[:, :, :, 1:2])
+            nc.scalar.copy(out=u[:, :, :, 13:13 + nf], in_=few[:, :, :, :, 0])
+            nc.scalar.copy(out=u[:, :, :, 13 + nf:23], in_=pairs[:, :, :, 0:10 - nf, 0])
+            nc.scalar.copy(out=u[:, :, :, 23:23 + nf], in_=few[:, :, :, :, 0])
+            nc.scalar.copy(out=u[:, :, :, 23 + nf:34], in_=pairs[:, :, :, 0:11 - nf, 0])
+            nc.scalar.copy(out=u[:, :, :, 34:34 + nf], in_=few[:, :, :, :, 1])
+            nc.scalar.copy(out=u[:, :, :, 34 + nf:45], in_=pairs[:, :, :, 0:11 - nf, 1])
+            nc.vector.tensor_tensor(out=u[:], in0=u[:], in1=pb_bc[:].unsqueeze(2).to_broadcast(shape), op=ALU.add)
+            f = tap_pool.tile(shape, F32, name="f")
+            nc.scalar.activation(out=f[:], in_=u[:], func=ACTF.Exp)
+            nc.scalar.activation(out=u[:], in_=u[:], func=ACTF.Relu)
+            nc.vector.scalar_tensor_tensor(out=f[:].rearrange("p h t k -> p (h t k)"),
+                                           in0=f[:].rearrange("p h t k -> p (h t k)"), scalar=1.0,
+                                           in1=u[:].rearrange("p h t k -> p (h t k)"), op0=ALU.min, op1=ALU.add)
+            gain = tap_pool.tile(shape, F32, name="gain")
+            for tau in range(4):
+                nc.scalar.activation(out=gain[:, :, :, 1 + NS * tau:1 + NS * (tau + 1)],
+                                     in_=g_raw[:, b, :, cc * TPC:(cc + 1) * TPC, :], func=ACTF.Copy, scale=D4[tau])
+            nc.scalar.copy(out=gain[:, :, :, 0:1],
+                           in_=bypass[:].unsqueeze(2).unsqueeze(3).to_broadcast([P, H, TPC, 1]))
+            w_tap = tap_pool.tile(shape, F32, name="w_tap")
+            nc.vector.tensor_tensor(out=w_tap[:], in0=f[:], in1=gain[:], op=ALU.mult)
+            z = tap_pool.tile([P, H, TPC], F32, name="z")
+            rz = tap_pool.tile([P, H, TPC], F32, name="rz")
+            nc.vector.tensor_reduce(out=z[:], in_=w_tap[:], axis=AX.X, op=ALU.add)
+            nc.vector.tensor_reduce(out=rz[:], in_=w_tap[:, :, :, 34:45], axis=AX.X, op=ALU.add)
+            nc.vector.scalar_tensor_tensor(out=z[:], in0=rz[:], scalar=-2.0, in1=z[:], op0=ALU.mult, op1=ALU.add)
+            nc.vector.tensor_scalar_add(out=z[:], in0=z[:], scalar1=1e-6)
+            nc.vector.reciprocal(out=rz[:], in_=z[:])
+            w_zero = tap_pool.tile([P, H, TPC], F32, name="w_zero")
+            nc.vector.tensor_reduce(out=w_zero[:], in_=w_tap[:, :, :, 0:12], axis=AX.X, op=ALU.add)
+            w_pow = tap_pool.tile([P, H, TPC, 10], F32, name="w_pow")
+            nc.vector.tensor_tensor(out=w_pow[:], in0=w_tap[:, :, :, 13:23], in1=w_tap[:, :, :, 23:33], op=ALU.add)
+
+            def of_place(s):
+                if s == 0:
+                    return w_zero[:]
+                if s == 1:
+                    return w_tap[:, :, :, 12]
+                if s % 2 == 1:
+                    return w_tap[:, :, :, 34 + (s - 3) // 2]
+                if s == NOFF - 2:
+                    return w_tap[:, :, :, 33]
+                return w_pow[:, :, :, s // 2 - 1]
+
+            weight_of[c] = (of_place, rz)
+
+        def skew(c):
+            of_place = weight_of[c][0]
+            for s in range(NEAR):
+                nc.scalar.copy(out=rows[:, :, :, P - OFFS[s]], in_=of_place(s))
+            for h in range(H):
+                area = scratch[SCR0 + h * TPC * UNIT:SCR0 + (h + 1) * TPC * UNIT]
+                nc.sync.dma_start(out=area.rearrange("(t p w) -> p t w", t=TPC, p=P), in_=rows[:, h, :, :])
+                skewed_of[(c, h)] = band_pool.tile([P, TPC, 2 * P], F32, name="skewed")
+                nc.sync.dma_start(out=skewed_of[(c, h)][:],
+                                  in_=area.rearrange("(t r) -> t r", t=TPC)[:, 0:2 * P * P]
+                                  .rearrange("t (p m) -> p t m", p=P))
+
+        def band(c, h):
+            band_of[(c, h)] = band_pool.tile([P, 2 * TPC, P], F32, name="band")
+            for half in range(2):
+                tr = ps_tr.tile([P, 4, P], F32, name="band_tr", tag="tr")
+                for i in range(4):
+                    tl, kb = divmod(4 * half + i, 2)
+                    nc.tensor.transpose(out=tr[:, i, :], in_=skewed_of[(c, h)][:, tl, kb * P:(kb + 1) * P],
+                                        identity=ident[:])
+                nc.scalar.copy(out=band_of[(c, h)][:, 4 * half:4 * half + 4, :], in_=tr[:])
+
+        def values(c, h):
+            b, cc = divmod(c, NCC)
+            of_place, rz = weight_of[c]
+            hs = slice(h * HD, (h + 1) * HD)
+            if h == 0:
+                if c >= HOLD0:
+                    o_of[c] = held[:, (c - HOLD0) * TPC:(c - HOLD0 + 1) * TPC, :]
+                else:
+                    o_of[c] = out_pool.tile([P, TPC, E], F32, name="o_sb")
+            o_sb = o_of[c]
+            near = ps_near.tile([P, TPC, HD], F32, name="near")
+            for tl in range(TPC):
+                blocks = [kb for kb in range(2) if cc * TPC + tl - 1 + kb >= 0]
+                for kb in blocks:
+                    nc.tensor.matmul(out=near[:, tl, :], lhsT=band_of[(c, h)][:, 2 * tl + kb, :],
+                                     rhs=v_tok[:, (c * TPC + tl - 1 + kb) % VRING, hs],
+                                     start=(kb == blocks[0]), stop=(kb == 1))
+            total = [near[:, tl, :] for tl in range(TPC)]
+            for s in range(NEAR, NOFF):
+                for tl in range(TPC):
+                    g = c * TPC + tl
+                    if s < n_valid(cc * TPC + tl):
+                        if OFFS[s] % P == 0:
+                            shifted = v_tok[:, (g - OFFS[s] // P) % VRING, hs]
+                        else:
+                            shifted = v_half[:, (g - 1) % BRING, hs]
+                        nc.vector.scalar_tensor_tensor(out=o_sb[:, tl, hs], in0=shifted,
+                                                       scalar=of_place(s)[:, h, tl:tl + 1], in1=total[tl],
+                                                       op0=ALU.mult, op1=ALU.add)
+                        total[tl] = o_sb[:, tl, hs]
+            for tl in range(TPC):
+                nc.scalar.activation(out=o_sb[:, tl, hs], in_=total[tl], func=ACTF.Copy, scale=rz[:, h, tl:tl + 1])
+            if h == H - 1 and c < HOLD0:
+                nc.sync.dma_start(out=out[b, cc * CH:(cc + 1) * CH, :].rearrange("(t p) e -> p t e", p=P),
+                                  in_=o_sb[:])
+
+        def is_chunk(c):
+            return 0 <= c < NCHUNK
+
+        load_x(0)
+        load_x(1)
+        for c in range(-2, NCHUNK + 3):
+            for tl in range(TPC):
+                if tl == 0 and is_chunk(c + 3) and c + 3 >= 2:
+                    load_x(c + 3)
+                if is_chunk(c + 2):
+                    transpose_x(c + 2, tl)
+                if is_chunk(c + 1):
+                    if tl == 0:
+                        quantise_x(c + 1)
+                    if tl == 1:
+                        project_kv(c + 1)
+                    if tl == 2:
+                        project_q(c + 1)
+                        turn_kv(c + 1)
+                if is_chunk(c):
+                    scores(c, tl)
+                if tl == 1 and is_chunk(c - 1):
+                    weights(c - 1)
+                    skew(c - 1)
+                if tl == 3 and is_chunk(c - 1):
+                    band(c - 1, 0)
+                if tl == 0 and is_chunk(c - 2):
+                    band(c - 2, 1)
+                    values(c - 2, 0)
+                if tl == 1 and is_chunk(c - 2):
+                    values(c - 2, 1)
+        for c in range(HOLD0, NCHUNK):
+            b, cc = divmod(c, NCC)
+            nc.sync.dma_start(out=out[b, cc * CH:(cc + 1) * CH, :].rearrange("(t p) e -> p t e", p=P),
+                              in_=held[:, (c - HOLD0) * TPC:(c - HOLD0 + 1) * TPC, :])

@@ -21,29 +21,33 @@ NCC = N // CH
 NT = N // P
 NCHUNK = B * NCC
 D4 = (0.4829629131445341, 0.8365163037378079, 0.2241438680420134, -0.1294095225512604)
-OFFS = tuple(sorted([0] + [1 << i for i in range(12)] + [3 << j for j in range(11)]))
+NPOW, NTRI = 12, 11
+OFFS = (0,) + tuple(1 << i for i in range(NPOW)) + tuple(3 << j for j in range(NTRI))
 NOFF = len(OFFS)
-NTAP = 1 + 4 * NS
-NEAR = 15
+RISING = sorted(range(NOFF), key=lambda s: OFFS[s])
+NEAR = [s for s in RISING if OFFS[s] <= P]
+FAR = [s for s in RISING if OFFS[s] > P]
+WHOLE = [s for s in range(NOFF) if OFFS[s] % P == 0]
+CUT = [s for s in range(NOFF) if OFFS[s] % P != 0]
 NFEW = 6
-KWIN = 256
-VWIN = 64
+TAP0, TAP1, TAP2, TAP3 = 1, 12, 24, 36
+NTAP = 47
+TAP_AT = (TAP0, TAP1, TAP2 + 1, TAP3)
+KPAD = P
+VPAD = 64
+GCH = 4
 ROW = 2 * P + 1
 UNIT = P * ROW
-VRING = 48
+VRING = 36
 BRING = 16
 SCR0 = B * N * E - H * TPC * UNIT
 HOLD0 = SCR0 // (CH * E)
 FLOPS = 2 * B * N * D * 3 * E + 4 * B * H * N * HD * NOFF
 
 
-def n_valid(t):
-    return len([o for o in OFFS if o <= t * P + P - 1])
-
-
-def cut_groups(nv):
-    cut = [s for s in range(nv) if OFFS[s] % P != 0]
-    return [cut[i:i + 4] for i in range(0, len(cut), 4)]
+def dead_tiles(cc, s):
+    first = max(0, -((P - 1 - OFFS[s]) // P))
+    return min(TPC, max(0, first - cc * TPC))
 
 
 def runs_of(places):
@@ -62,7 +66,8 @@ def tile_dwarfattention_pa_t_kernel(tc, x, W_qkv, b_qkv, gains, pos_bias, identi
         const = ctx.enter_context(tc.tile_pool(name="const", bufs=1))
         ps_tr = ctx.enter_context(tc.psum_pool(name="ps_tr", bufs=2))
         ps_mx = ctx.enter_context(tc.psum_pool(name="ps_mx", bufs=1))
-        ps_cut = ctx.enter_context(tc.psum_pool(name="ps_cut", bufs=4))
+        ps_q = ctx.enter_context(tc.psum_pool(name="ps_q", bufs=1))
+        ps_cut = ctx.enter_context(tc.psum_pool(name="ps_cut", bufs=3))
         ps_near = ctx.enter_context(tc.psum_pool(name="ps_near", bufs=1))
 
         ident = const.tile([P, P], F32, name="ident")
@@ -70,9 +75,10 @@ def tile_dwarfattention_pa_t_kernel(tc, x, W_qkv, b_qkv, gains, pos_bias, identi
         w_codes = const.tile([P, 2, 3 * P], U32, name="w_codes", align_bytes=64)
         w_scales = const.tile([P, 2, 3 * P], U8, name="w_scales", align_bytes=64)
         bias_col = const.tile([P, 4], F32, name="bias_col")
-        pb_bc = const.tile([P, H, NTAP], F32, name="pb_bc")
+        pb_bc = const.tile([P, NTAP, H], F32, name="pb_bc")
         g_raw = const.tile([P, B, H, NT, NS], BF16, name="g_raw")
         bypass = const.tile([P, H], F32, name="bypass")
+        k_f = const.tile([P, KPAD + N], F32, name="k_f")
         k_tok = const.tile([P, NT, E], F32, name="k_tok")
         v_tok = const.tile([P, VRING, E], F32, name="v_tok")
         v_half = const.tile([P, BRING, E], F32, name="v_half")
@@ -80,6 +86,8 @@ def tile_dwarfattention_pa_t_kernel(tc, x, W_qkv, b_qkv, gains, pos_bias, identi
         spare = const.tile([P, HD], F32, name="spare")
         rows = const.tile([P, H, TPC, ROW], F32, name="rows")
         nc.gpsimd.memset(rows[:], 0.0)
+        nc.gpsimd.memset(k_f[:, 0:KPAD], 0.0)
+        nc.gpsimd.memset(pb_bc[:], 0.0)
 
         with tc.tile_pool(name="setup", bufs=1) as setup:
             w_sb = setup.tile([P, 3, D], BF16, name="w_sb")
@@ -118,9 +126,9 @@ def tile_dwarfattention_pa_t_kernel(tc, x, W_qkv, b_qkv, gains, pos_bias, identi
             nc.tensor.transpose(out=b_tr[:, 0, :], in_=b_rows32[:], identity=ident[:])
             nc.vector.tensor_copy(out=bias_col[:, 0:3], in_=b_tr[:, 0, 0:3])
 
-            nc.vector.memset(pb_bc[:], 0.0)
-            nc.vector.tensor_copy(out=pb_bc[:, :, 1:NTAP].rearrange("p h (t j) -> p h t j", t=4),
-                                  in_=pb_raw[:].rearrange("p (j t h) -> p h t j", t=4, h=H))
+            pb_view = pb_raw[:].rearrange("p (j t h) -> p t j h", t=4, h=H)
+            for tau in range(4):
+                nc.vector.tensor_copy(out=pb_bc[:, TAP_AT[tau]:TAP_AT[tau] + NS, :], in_=pb_view[:, tau, :, :])
 
             ib = setup.tile([P, H], F32, name="ib")
             nc.vector.tensor_copy(out=ib[:], in_=ib_raw[:])
@@ -132,28 +140,37 @@ def tile_dwarfattention_pa_t_kernel(tc, x, W_qkv, b_qkv, gains, pos_bias, identi
             nc.vector.scalar_tensor_tensor(out=bypass[:], in0=ib[:], scalar=0.0, in1=ib_e[:],
                                            op0=ALU.max, op1=ALU.add)
 
+
         x_pool = ctx.enter_context(tc.tile_pool(name="x_pool", bufs=2))
         grouped_pool = ctx.enter_context(tc.tile_pool(name="grouped_pool", bufs=2))
         code_pool = ctx.enter_context(tc.tile_pool(name="code_pool", bufs=2))
-        kf_pool = ctx.enter_context(tc.tile_pool(name="kf_pool", bufs=3))
-        vf_pool = ctx.enter_context(tc.tile_pool(name="vf_pool", bufs=3))
-        q_pool = ctx.enter_context(tc.tile_pool(name="q_pool", bufs=3))
-        prod_pool = ctx.enter_context(tc.tile_pool(name="prod_pool", bufs=3))
+        gain_pool = ctx.enter_context(tc.tile_pool(name="gain_pool", bufs=2))
+        vf_pool = ctx.enter_context(tc.tile_pool(name="vf_pool", bufs=2))
+        q_pool = ctx.enter_context(tc.tile_pool(name="q_pool", bufs=2))
+        whole_pool = ctx.enter_context(tc.tile_pool(name="whole_pool", bufs=1))
+        cut_pool = ctx.enter_context(tc.tile_pool(name="cut_pool", bufs=3))
         score_pool = ctx.enter_context(tc.tile_pool(name="score_pool", bufs=3))
-        tap_pool = ctx.enter_context(tc.tile_pool(name="tap_pool", bufs=3))
+        tap_pool = ctx.enter_context(tc.tile_pool(name="tap_pool", bufs=2))
+        weight_pool = ctx.enter_context(tc.tile_pool(name="weight_pool", bufs=3))
         band_pool = ctx.enter_context(tc.tile_pool(name="band_pool", bufs=2))
+        far_pool = ctx.enter_context(tc.tile_pool(name="far_pool", bufs=2))
         out_pool = ctx.enter_context(tc.tile_pool(name="out_pool", bufs=2))
 
-        x_of, grouped_of, code_of = {}, {}, {}
-        kf_of, vf_of, q_of = {}, {}, {}
-        score_of, weight_of, skewed_of, band_of, o_of = {}, {}, {}, {}, {}
+        x_of, grouped_of, code_of, q_of, vf_of, whole_of, gain_of = {}, {}, {}, {}, {}, {}, {}
+        q_ps_of, score_of, weight_of, skewed_of, band_of, far_of, near_of = {}, {}, {}, {}, {}, {}, {}
         scratch = out.rearrange("b n e -> (b n e)")
 
-        def feature_major(c):
-            if c not in kf_of:
-                kf_of[c] = kf_pool.tile([P, KWIN + CH], F32, name="kf")
-                vf_of[c] = vf_pool.tile([P, VWIN + CH], F32, name="vf")
-            return kf_of[c], vf_of[c]
+        def make_gain(c, tau):
+            b, cc = divmod(c, NCC)
+            n = GCH * TPC
+            if tau == 0:
+                gain_of[c // GCH] = gain_pool.tile([P, n, NTAP, H], F32, name="gain")
+                nc.gpsimd.memset(gain_of[c // GCH][:, :, TAP2 - 1:TAP2 + 1, :], 0.0)
+                nc.scalar.copy(out=gain_of[c // GCH][:, :, 0, :],
+                               in_=bypass[:].unsqueeze(1).to_broadcast([P, n, H]))
+            for h in range(H):
+                nc.scalar.activation(out=gain_of[c // GCH][:, :, TAP_AT[tau]:TAP_AT[tau] + NS, h],
+                                     in_=g_raw[:, b, h, cc * TPC:cc * TPC + n, :], func=ACTF.Copy, scale=D4[tau])
 
         def load_x(c):
             b, cc = divmod(c, NCC)
@@ -182,7 +199,7 @@ def tile_dwarfattention_pa_t_kernel(tc, x, W_qkv, b_qkv, gains, pos_bias, identi
                     in_=grouped_of[c][:, g, :, :].rearrange("p r u -> p (r u)").bitcast(BF16))
             code_of[c] = (codes, scales)
 
-        def project(c, f):
+        def project(c, f, dst):
             codes, scales = code_of[c]
             acc = ps_mx.tile([P, CH], F32, name="acc", tag="mx")
             for g in range(2):
@@ -190,135 +207,131 @@ def tile_dwarfattention_pa_t_kernel(tc, x, W_qkv, b_qkv, gains, pos_bias, identi
                                     lhsT_scale=w_scales[:, g, f * P:(f + 1) * P],
                                     rhs=codes[:, g, :].bitcast(FP8X4), rhs_scale=scales[:, g, :],
                                     start=(g == 0), stop=(g == 1))
-            return acc
+            nc.scalar.activation(out=dst, in_=acc[:], func=ACTF.Identity, bias=bias_col[:, f:f + 1], scale=1.0)
 
-        def add_bias(dst, acc, f):
-            nc.scalar.activation(out=dst, in_=acc, func=ACTF.Identity, bias=bias_col[:, f:f + 1], scale=1.0)
+        def project_all(c):
+            first = (c % NCC) * CH
+            project(c, 1, k_f[:, KPAD + first:KPAD + first + CH])
+            q_f = q_pool.tile([P, CH], F32, name="q_f")
+            project(c, 0, q_f[:])
+            vf_of[c] = vf_pool.tile([P, VPAD + CH], F32, name="v_f")
+            if c % NCC == 0:
+                nc.gpsimd.memset(vf_of[c][:, 0:VPAD], 0.0)
+            else:
+                nc.scalar.copy(out=vf_of[c][:, 0:VPAD], in_=vf_of[c - 1][:, CH:CH + VPAD])
+            project(c, 2, vf_of[c][:, VPAD:VPAD + CH])
+            q_of[c] = q_pool.tile([P, TPC, E], F32, name="q_tok")
+            q_ps_of[c] = ps_q.tile([P, TPC, P], F32, name="q_ps")
+            token_major(q_f, 0, q_of[c][:], q_ps_of[c])
 
-        def project_kv(c):
-            cc = c % NCC
-            for f, win in ((1, KWIN), (2, VWIN)):
-                dst = feature_major(c)[f - 1]
-                if cc == 0:
-                    nc.vector.memset(dst[:, 0:win], 0.0)
-                acc = project(c, f)
-                add_bias(dst[:, win:win + CH], acc[:], f)
-                if cc + 1 < NCC:
-                    add_bias(feature_major(c + 1)[f - 1][:, 0:win], acc[:, CH - win:CH], f)
-
-        def token_major(src, first, dst):
-            tr = ps_tr.tile([P, TPC, P], F32, name="tok_tr", tag="tr")
+        def token_major(src, first, dst, tr=None):
+            if tr is None:
+                tr = ps_tr.tile([P, TPC, P], F32, name="tok_tr", tag="tr")
             for tl in range(TPC):
                 nc.tensor.transpose(out=tr[:, tl, :], in_=src[:, first + tl * P:first + (tl + 1) * P],
                                     identity=ident[:])
             nc.scalar.copy(out=dst, in_=tr[:])
 
-        def project_q(c):
-            q_f = q_pool.tile([P, CH], F32, name="q_f")
-            add_bias(q_f[:], project(c, 0)[:], 0)
-            q_of[c] = q_pool.tile([P, TPC, E], F32, name="q_tok")
-            token_major(q_f, 0, q_of[c][:])
-
         def turn_kv(c):
-            cc = c % NCC
+            t0 = (c % NCC) * TPC
+            token_major(k_f, KPAD + t0 * P, k_tok[:, t0:t0 + TPC, :])
             g0 = c * TPC
-            token_major(kf_of[c], KWIN, k_tok[:, cc * TPC:(cc + 1) * TPC, :])
-            token_major(vf_of[c], VWIN, v_tok[:, g0 % VRING:g0 % VRING + TPC, :])
+            token_major(vf_of[c], VPAD, v_tok[:, g0 % VRING:g0 % VRING + TPC, :])
             token_major(vf_of[c], 0, v_half[:, g0 % BRING:g0 % BRING + TPC, :])
 
         def scores(c, tl):
             cc = c % NCC
+            t0 = cc * TPC
             if tl == 0:
-                s_all = score_pool.tile([P, H, TPC, NOFF], F32, name="s_all")
-                s_few = score_pool.tile([P, H, TPC, NFEW], F32, name="s_few")
-                score_of[c] = (s_all, s_few)
-                if n_valid(cc * TPC) < NOFF:
-                    nc.vector.memset(s_all[:], 0.0)
-            s_all, s_few = score_of[c]
-            t = cc * TPC + tl
-            nv = n_valid(t)
+                score_of[c] = score_pool.tile([P, TPC, NOFF, H], F32, name="score")
+                whole_of[c] = whole_pool.tile([P, len(WHOLE), TPC, E], F32, name="whole")
+                if any(dead_tiles(cc, s) for s in range(NOFF)):
+                    nc.vector.memset(score_of[c][:], 0.0)
+            score, whole = score_of[c], whole_of[c]
             q_t = q_of[c][:, tl, :]
-            prod = prod_pool.tile([P, NOFF, E], F32, name="prod")
-            for places in cut_groups(nv):
+            places = [s for s in CUT if dead_tiles(cc, s) <= tl]
+            prod = cut_pool.tile([P, len(CUT), E], F32, name="prod")
+            for g in range(0, len(places), 4):
                 cut = ps_cut.tile([P, 4, P], F32, name="cut", tag="cut")
-                for i, s in enumerate(places):
-                    first = KWIN + tl * P - OFFS[s]
-                    nc.tensor.transpose(out=cut[:, i, :], in_=kf_of[c][:, first:first + P], identity=ident[:])
-                for i0, s0, ln in runs_of(places):
-                    nc.vector.tensor_tensor(out=prod[:, s0:s0 + ln, :], in0=cut[:, i0:i0 + ln, :],
-                                            in1=q_t.unsqueeze(1).to_broadcast([P, ln, E]), op=ALU.mult)
-            for s in range(nv):
-                if OFFS[s] % P == 0:
-                    nc.vector.tensor_tensor(out=prod[:, s, :], in0=k_tok[:, t - OFFS[s] // P, :], in1=q_t,
-                                            op=ALU.mult)
-            for s in range(NFEW):
-                for h in range(H):
-                    nc.scalar.activation(out=spare[:], in_=prod[:, s, h * HD:(h + 1) * HD], func=ACTF.Copy,
-                                         accum_out=s_few[:, h, tl, s:s + 1])
-            nc.vector.tensor_reduce(out=s_all[:, :, tl, NFEW:nv].rearrange("p h s -> p s h"),
-                                    in_=prod[:, NFEW:nv, :].rearrange("p s (h d) -> p s h d", h=H),
-                                    axis=AX.X, op=ALU.add)
+                for i, s in enumerate(places[g:g + 4]):
+                    first = KPAD + (t0 + tl) * P - OFFS[s]
+                    nc.tensor.transpose(out=cut[:, i, :], in_=k_f[:, first:first + P], identity=ident[:])
+                n = len(places[g:g + 4])
+                nc.vector.tensor_tensor(out=prod[:, g:g + n, :], in0=cut[:, 0:n, :],
+                                        in1=q_t.unsqueeze(1).to_broadcast([P, n, E]), op=ALU.mult)
+            for i in range(tl, len(WHOLE), 2) if tl < 2 else ():
+                s = WHOLE[i]
+                dead = dead_tiles(cc, s)
+                if dead < TPC:
+                    first = t0 - OFFS[s] // P
+                    nc.vector.tensor_tensor(out=whole[:, i, dead:TPC, :], in0=k_tok[:, first + dead:first + TPC, :],
+                                            in1=q_ps_of[c][:, dead:TPC, :], op=ALU.mult)
+            for i, s in enumerate(places):
+                if s < NFEW:
+                    for h in range(H):
+                        nc.scalar.activation(out=spare[:], in_=prod[:, i, h * HD:(h + 1) * HD], func=ACTF.Copy,
+                                             accum_out=score[:, tl, s, h:h + 1])
+            for i, s, ln in runs_of(places):
+                skip = max(0, NFEW - s)
+                nc.vector.tensor_reduce(out=score[:, tl, s + skip:s + ln, :],
+                                        in_=prod[:, i + skip:i + ln, :].rearrange("p s (h d) -> p s h d", h=H),
+                                        axis=AX.X, op=ALU.add)
+            if tl == 2:
+                for t in range(TPC):
+                    for h in range(H):
+                        nc.scalar.activation(out=spare[:], in_=whole[:, 0, t, h * HD:(h + 1) * HD], func=ACTF.Copy,
+                                             accum_out=score[:, t, 0, h:h + 1])
+                for dead in range(TPC):
+                    live = [s for s in WHOLE if s >= NFEW and dead_tiles(cc, s) == dead]
+                    for j, s, ln in runs_of(live):
+                        i = WHOLE.index(s)
+                        nc.vector.tensor_reduce(
+                            out=score[:, dead:TPC, s:s + ln, :].rearrange("p t s h -> p s t h"),
+                            in_=whole[:, i:i + ln, dead:TPC, :].rearrange("p s t (h d) -> p s t h d", h=H),
+                            axis=AX.X, op=ALU.add)
 
         def weights(c):
-            b, cc = divmod(c, NCC)
-            s_all, s_few = score_of[c]
-            shape = [P, H, TPC, NTAP]
-            nf = (NFEW - 2) // 2
-            few = s_few[:, :, :, 2:NFEW].rearrange("p h t (i two) -> p h t i two", two=2)
-            pairs = s_all[:, :, :, NFEW:NOFF].rearrange("p h t (i two) -> p h t i two", two=2)
-            u = tap_pool.tile(shape, F32, name="u")
-            nc.scalar.copy(out=u[:, :, :, 0:12], in_=s_few[:, :, :, 0:1].to_broadcast([P, H, TPC, 12]))
-            nc.scalar.copy(out=u[:, :, :, 12:13], in_=s_few[:, :, :, 1:2])
-            nc.scalar.copy(out=u[:, :, :, 13:13 + nf], in_=few[:, :, :, :, 0])
-            nc.scalar.copy(out=u[:, :, :, 13 + nf:23], in_=pairs[:, :, :, 0:10 - nf, 0])
-            nc.scalar.copy(out=u[:, :, :, 23:23 + nf], in_=few[:, :, :, :, 0])
-            nc.scalar.copy(out=u[:, :, :, 23 + nf:34], in_=pairs[:, :, :, 0:11 - nf, 0])
-            nc.scalar.copy(out=u[:, :, :, 34:34 + nf], in_=few[:, :, :, :, 1])
-            nc.scalar.copy(out=u[:, :, :, 34 + nf:45], in_=pairs[:, :, :, 0:11 - nf, 1])
-            nc.vector.tensor_tensor(out=u[:], in0=u[:], in1=pb_bc[:].unsqueeze(2).to_broadcast(shape), op=ALU.add)
-            f = tap_pool.tile(shape, F32, name="f")
+            score = score_of[c]
+            u = tap_pool.tile([P, TPC, NTAP, H], F32, name="u")
+            nc.vector.tensor_tensor(out=u[:, :, 0:TAP1, :], in0=score[:, :, 0:1, :].to_broadcast([P, TPC, TAP1, H]),
+                                    in1=pb_bc[:, 0:TAP1, :].unsqueeze(1).to_broadcast([P, TPC, TAP1, H]), op=ALU.add)
+            for tap, place, ln in ((TAP1, 1, NPOW), (TAP2, 1, NPOW), (TAP3, 1 + NPOW, NTRI)):
+                nc.vector.tensor_tensor(out=u[:, :, tap:tap + ln, :], in0=score[:, :, place:place + ln, :],
+                                        in1=pb_bc[:, tap:tap + ln, :].unsqueeze(1).to_broadcast([P, TPC, ln, H]),
+                                        op=ALU.add)
+            f = tap_pool.tile([P, TPC, NTAP, H], F32, name="f")
             nc.scalar.activation(out=f[:], in_=u[:], func=ACTF.Exp)
             nc.scalar.activation(out=u[:], in_=u[:], func=ACTF.Relu)
-            nc.vector.scalar_tensor_tensor(out=f[:].rearrange("p h t k -> p (h t k)"),
-                                           in0=f[:].rearrange("p h t k -> p (h t k)"), scalar=1.0,
-                                           in1=u[:].rearrange("p h t k -> p (h t k)"), op0=ALU.min, op1=ALU.add)
-            gain = tap_pool.tile(shape, F32, name="gain")
-            for tau in range(4):
-                nc.scalar.activation(out=gain[:, :, :, 1 + NS * tau:1 + NS * (tau + 1)],
-                                     in_=g_raw[:, b, :, cc * TPC:(cc + 1) * TPC, :], func=ACTF.Copy, scale=D4[tau])
-            nc.scalar.copy(out=gain[:, :, :, 0:1],
-                           in_=bypass[:].unsqueeze(2).unsqueeze(3).to_broadcast([P, H, TPC, 1]))
-            w_tap = tap_pool.tile(shape, F32, name="w_tap")
-            nc.vector.tensor_tensor(out=w_tap[:], in0=f[:], in1=gain[:], op=ALU.mult)
-            z = tap_pool.tile([P, H, TPC], F32, name="z")
-            rz = tap_pool.tile([P, H, TPC], F32, name="rz")
-            nc.vector.tensor_reduce(out=z[:], in_=w_tap[:], axis=AX.X, op=ALU.add)
-            nc.vector.tensor_reduce(out=rz[:], in_=w_tap[:, :, :, 34:45], axis=AX.X, op=ALU.add)
-            nc.vector.scalar_tensor_tensor(out=z[:], in0=rz[:], scalar=-2.0, in1=z[:], op0=ALU.mult, op1=ALU.add)
-            nc.vector.tensor_scalar_add(out=z[:], in0=z[:], scalar1=1e-6)
+            nc.vector.scalar_tensor_tensor(out=f[:], in0=f[:], scalar=1.0, in1=u[:], op0=ALU.min, op1=ALU.add)
+            w_tap = tap_pool.tile([P, TPC, TAP3, H], F32, name="w_tap")
+            w = weight_pool.tile([P, TPC, NOFF, H], F32, name="w")
+            first = (c % GCH) * TPC
+            g_c = gain_of[c // GCH][:, first:first + TPC, :, :]
+            nc.vector.tensor_tensor(out=w_tap[:], in0=f[:, :, 0:TAP3, :], in1=g_c[:, :, 0:TAP3, :], op=ALU.mult)
+            nc.vector.tensor_tensor(out=w[:, :, 1 + NPOW:NOFF, :], in0=f[:, :, TAP3:NTAP, :],
+                                    in1=g_c[:, :, TAP3:NTAP, :], op=ALU.mult)
+            nc.vector.tensor_reduce(out=w[:, :, 0, :], in_=w_tap[:, :, 0:TAP1, :].rearrange("p t k h -> p t h k"),
+                                    axis=AX.X, op=ALU.add)
+            nc.vector.tensor_tensor(out=w[:, :, 1:1 + NPOW, :], in0=w_tap[:, :, TAP1:TAP2, :],
+                                    in1=w_tap[:, :, TAP2:TAP3, :], op=ALU.add)
+            z = weight_pool.tile([P, TPC, H], F32, name="z")
+            z_tri = weight_pool.tile([P, TPC, H], F32, name="z_tri")
+            nc.vector.tensor_reduce(out=z[:], in_=w[:, :, 0:1 + NPOW, :].rearrange("p t s h -> p t h s"),
+                                    axis=AX.X, op=ALU.add)
+            nc.vector.tensor_reduce(out=z_tri[:], in_=w[:, :, 1 + NPOW:NOFF, :].rearrange("p t s h -> p t h s"),
+                                    axis=AX.X, op=ALU.add)
+            nc.vector.scalar_tensor_tensor(out=z[:], in0=z[:], scalar=1e-6, in1=z_tri[:], op0=ALU.add,
+                                           op1=ALU.subtract)
+            rz = weight_pool.tile([P, TPC, H], F32, name="rz")
             nc.vector.reciprocal(out=rz[:], in_=z[:])
-            w_zero = tap_pool.tile([P, H, TPC], F32, name="w_zero")
-            nc.vector.tensor_reduce(out=w_zero[:], in_=w_tap[:, :, :, 0:12], axis=AX.X, op=ALU.add)
-            w_pow = tap_pool.tile([P, H, TPC, 10], F32, name="w_pow")
-            nc.vector.tensor_tensor(out=w_pow[:], in0=w_tap[:, :, :, 13:23], in1=w_tap[:, :, :, 23:33], op=ALU.add)
-
-            def of_place(s):
-                if s == 0:
-                    return w_zero[:]
-                if s == 1:
-                    return w_tap[:, :, :, 12]
-                if s % 2 == 1:
-                    return w_tap[:, :, :, 34 + (s - 3) // 2]
-                if s == NOFF - 2:
-                    return w_tap[:, :, :, 33]
-                return w_pow[:, :, :, s // 2 - 1]
-
-            weight_of[c] = (of_place, rz)
+            nc.vector.tensor_tensor(out=w[:], in0=w[:], in1=rz[:].unsqueeze(2).to_broadcast([P, TPC, NOFF, H]),
+                                    op=ALU.mult)
+            weight_of[c] = w
 
         def skew(c):
-            of_place = weight_of[c][0]
-            for s in range(NEAR):
-                nc.scalar.copy(out=rows[:, :, :, P - OFFS[s]], in_=of_place(s))
+            w = weight_of[c]
+            for s in NEAR:
+                nc.scalar.copy(out=rows[:, :, :, P - OFFS[s]], in_=w[:, :, s, :].rearrange("p t h -> p h t"))
             for h in range(H):
                 area = scratch[SCR0 + h * TPC * UNIT:SCR0 + (h + 1) * TPC * UNIT]
                 nc.sync.dma_start(out=area.rearrange("(t p w) -> p t w", t=TPC, p=P), in_=rows[:, h, :, :])
@@ -337,41 +350,59 @@ def tile_dwarfattention_pa_t_kernel(tc, x, W_qkv, b_qkv, gains, pos_bias, identi
                                         identity=ident[:])
                 nc.scalar.copy(out=band_of[(c, h)][:, 4 * half:4 * half + 4, :], in_=tr[:])
 
-        def values(c, h):
-            b, cc = divmod(c, NCC)
-            of_place, rz = weight_of[c]
+        def ring_pieces(first, n, size):
+            at = first % size
+            head = min(n, size - at)
+            return [(0, at, head)] + ([(head, 0, n - head)] if head < n else [])
+
+        def far_values(c):
+            cc = c % NCC
+            far_of[c] = far_pool.tile([P, TPC, E], F32, name="far")
+            far = far_of[c]
+            for s in FAR:
+                dead = dead_tiles(cc, s)
+                if dead == TPC:
+                    continue
+                first = s == FAR[0]
+                if first and dead:
+                    nc.gpsimd.memset(far[:, 0:dead, :], 0.0)
+                part = far if first else far_pool.tile([P, TPC, E], F32, name="part")
+                if OFFS[s] % P == 0:
+                    ring, size, g = v_tok, VRING, c * TPC + dead - OFFS[s] // P
+                else:
+                    ring, size, g = v_half, BRING, c * TPC + dead - 1
+                for i, at, n in ring_pieces(g, TPC - dead, size):
+                    t = dead + i
+                    nc.gpsimd.tensor_tensor(
+                        out=part[:, t:t + n, :].rearrange("p t (h d) -> p t h d", h=H),
+                        in0=ring[:, at:at + n, :].rearrange("p t (h d) -> p t h d", h=H),
+                        in1=weight_of[c][:, t:t + n, s, :].unsqueeze(3).to_broadcast([P, n, H, HD]), op=ALU.mult)
+                if not first:
+                    nc.gpsimd.tensor_tensor(out=far[:, dead:TPC, :], in0=far[:, dead:TPC, :],
+                                            in1=part[:, dead:TPC, :], op=ALU.add)
+
+        def near_values(c, h):
+            cc = c % NCC
             hs = slice(h * HD, (h + 1) * HD)
             if h == 0:
-                if c >= HOLD0:
-                    o_of[c] = held[:, (c - HOLD0) * TPC:(c - HOLD0 + 1) * TPC, :]
-                else:
-                    o_of[c] = out_pool.tile([P, TPC, E], F32, name="o_sb")
-            o_sb = o_of[c]
-            near = ps_near.tile([P, TPC, HD], F32, name="near")
+                near_of[c] = ps_near.tile([P, TPC, E], F32, name="near")
             for tl in range(TPC):
                 blocks = [kb for kb in range(2) if cc * TPC + tl - 1 + kb >= 0]
                 for kb in blocks:
-                    nc.tensor.matmul(out=near[:, tl, :], lhsT=band_of[(c, h)][:, 2 * tl + kb, :],
+                    nc.tensor.matmul(out=near_of[c][:, tl, hs], lhsT=band_of[(c, h)][:, 2 * tl + kb, :],
                                      rhs=v_tok[:, (c * TPC + tl - 1 + kb) % VRING, hs],
                                      start=(kb == blocks[0]), stop=(kb == 1))
-            total = [near[:, tl, :] for tl in range(TPC)]
-            for s in range(NEAR, NOFF):
-                for tl in range(TPC):
-                    g = c * TPC + tl
-                    if s < n_valid(cc * TPC + tl):
-                        if OFFS[s] % P == 0:
-                            shifted = v_tok[:, (g - OFFS[s] // P) % VRING, hs]
-                        else:
-                            shifted = v_half[:, (g - 1) % BRING, hs]
-                        nc.vector.scalar_tensor_tensor(out=o_sb[:, tl, hs], in0=shifted,
-                                                       scalar=of_place(s)[:, h, tl:tl + 1], in1=total[tl],
-                                                       op0=ALU.mult, op1=ALU.add)
-                        total[tl] = o_sb[:, tl, hs]
-            for tl in range(TPC):
-                nc.scalar.activation(out=o_sb[:, tl, hs], in_=total[tl], func=ACTF.Copy, scale=rz[:, h, tl:tl + 1])
-            if h == H - 1 and c < HOLD0:
-                nc.sync.dma_start(out=out[b, cc * CH:(cc + 1) * CH, :].rearrange("(t p) e -> p t e", p=P),
-                                  in_=o_sb[:])
+
+        def finish(c):
+            b, cc = divmod(c, NCC)
+            if c >= HOLD0:
+                o_sb = held[:, (c - HOLD0) * TPC:(c - HOLD0 + 1) * TPC, :]
+            else:
+                o_tile = out_pool.tile([P, TPC, E], F32, name="o_tile")
+                o_sb = o_tile[:]
+            nc.vector.tensor_tensor(out=o_sb, in0=near_of[c][:], in1=far_of[c][:], op=ALU.add)
+            if c < HOLD0:
+                nc.sync.dma_start(out=out[b, cc * CH:(cc + 1) * CH, :].rearrange("(t p) e -> p t e", p=P), in_=o_sb)
 
         def is_chunk(c):
             return 0 <= c < NCHUNK
@@ -379,31 +410,34 @@ def tile_dwarfattention_pa_t_kernel(tc, x, W_qkv, b_qkv, gains, pos_bias, identi
         load_x(0)
         load_x(1)
         for c in range(-2, NCHUNK + 3):
-            for tl in range(TPC):
-                if tl == 0 and is_chunk(c + 3) and c + 3 >= 2:
+            for step in range(TPC):
+                if step == 0 and is_chunk(c + 3) and c + 3 >= 2:
                     load_x(c + 3)
                 if is_chunk(c + 2):
-                    transpose_x(c + 2, tl)
+                    transpose_x(c + 2, step)
                 if is_chunk(c + 1):
-                    if tl == 0:
+                    if step == 0:
                         quantise_x(c + 1)
-                    if tl == 1:
-                        project_kv(c + 1)
-                    if tl == 2:
-                        project_q(c + 1)
+                    if step == 1:
+                        project_all(c + 1)
+                    if step == 2:
                         turn_kv(c + 1)
                 if is_chunk(c):
-                    scores(c, tl)
-                if tl == 1 and is_chunk(c - 1):
+                    scores(c, step)
+                if c % GCH == 0 and is_chunk(c):
+                    make_gain(c, step)
+                if step == 0 and is_chunk(c - 1):
                     weights(c - 1)
                     skew(c - 1)
-                if tl == 3 and is_chunk(c - 1):
+                    far_values(c - 1)
+                if step == 3 and is_chunk(c - 1):
                     band(c - 1, 0)
-                if tl == 0 and is_chunk(c - 2):
+                if step == 0 and is_chunk(c - 2):
                     band(c - 2, 1)
-                    values(c - 2, 0)
-                if tl == 1 and is_chunk(c - 2):
-                    values(c - 2, 1)
+                    near_values(c - 2, 0)
+                if step == 1 and is_chunk(c - 2):
+                    near_values(c - 2, 1)
+                    finish(c - 2)
         for c in range(HOLD0, NCHUNK):
             b, cc = divmod(c, NCC)
             nc.sync.dma_start(out=out[b, cc * CH:(cc + 1) * CH, :].rearrange("(t p) e -> p t e", p=P),

@@ -89,19 +89,29 @@ def tile_dwarfattention_pa_t_kernel(tc, x, W_qkv, b_qkv, gains, pos_bias, identi
         nc.gpsimd.memset(k_f[:, 0:KPAD], 0.0)
         nc.gpsimd.memset(pb_bc[:], 0.0)
 
-        with tc.tile_pool(name="setup", bufs=1) as setup:
-            w_sb = setup.tile([P, 3, D], BF16, name="w_sb")
-            nc.sync.dma_start(out=w_sb[:], in_=W_qkv.rearrange("(f p) k -> p f k", p=P))
+        x_pool = ctx.enter_context(tc.tile_pool(name="x_pool", bufs=2))
+        grouped_pool = ctx.enter_context(tc.tile_pool(name="grouped_pool", bufs=2))
+        code_pool = ctx.enter_context(tc.tile_pool(name="code_pool", bufs=2))
+        x_of = {}
+
+        def load_x(c):
+            b, cc = divmod(c, NCC)
+            x_of[c] = x_pool.tile([P, TPC, D], BF16, name="x_sb")
+            nc.sync.dma_start(out=x_of[c][:],
+                              in_=x[b, cc * CH:(cc + 1) * CH, :].rearrange("(t p) k -> p t k", p=P))
+
+        with tc.manual_schedule(), tc.tile_pool(name="setup", bufs=1) as setup:
             b_rows = setup.tile([P, P], BF16, name="b_rows")
             nc.vector.memset(b_rows[:], 0.0)
-            nc.scalar.dma_start(out=b_rows[0:3, :], in_=b_qkv.rearrange("(f c) -> f c", c=P))
+            nc.sync.dma_start(out=b_rows[0:3, :], in_=b_qkv.rearrange("(f c) -> f c", c=P))
+            w_sb = setup.tile([P, 3, D], BF16, name="w_sb")
+            nc.sync.dma_start(out=w_sb[:], in_=W_qkv.rearrange("(f p) k -> p f k", p=P))
+            load_x(0)
             pb_raw = setup.tile([P, 4 * NS * H], BF16, name="pb_raw")
-            nc.scalar.dma_start(out=pb_raw[:], in_=pos_bias.rearrange("r h -> (r h)").partition_broadcast(P))
+            nc.sync.dma_start(out=pb_raw[:], in_=pos_bias.rearrange("r h -> (r h)").partition_broadcast(P))
             ib_raw = setup.tile([P, H], BF16, name="ib_raw")
-            nc.scalar.dma_start(out=ib_raw[:], in_=identity_bypass.partition_broadcast(P))
-            for b in range(B):
-                for h in range(H):
-                    nc.scalar.dma_start(out=g_raw[:, b, h, :, :], in_=gains[b, h].rearrange("(t p) j -> p t j", p=P))
+            nc.sync.dma_start(out=ib_raw[:], in_=identity_bypass.partition_broadcast(P))
+            load_x(1)
 
             w_grouped = setup.tile([P, 2, 3 * P, 2], F32, name="w_grouped", align_bytes=64)
             for f in range(3):
@@ -141,9 +151,7 @@ def tile_dwarfattention_pa_t_kernel(tc, x, W_qkv, b_qkv, gains, pos_bias, identi
                                            op0=ALU.max, op1=ALU.add)
 
 
-        x_pool = ctx.enter_context(tc.tile_pool(name="x_pool", bufs=2))
-        grouped_pool = ctx.enter_context(tc.tile_pool(name="grouped_pool", bufs=2))
-        code_pool = ctx.enter_context(tc.tile_pool(name="code_pool", bufs=2))
+        band_pool = ctx.enter_context(tc.tile_pool(name="band_pool", bufs=2))
         gain_pool = ctx.enter_context(tc.tile_pool(name="gain_pool", bufs=2))
         vf_pool = ctx.enter_context(tc.tile_pool(name="vf_pool", bufs=2))
         q_pool = ctx.enter_context(tc.tile_pool(name="q_pool", bufs=2))
@@ -152,13 +160,16 @@ def tile_dwarfattention_pa_t_kernel(tc, x, W_qkv, b_qkv, gains, pos_bias, identi
         score_pool = ctx.enter_context(tc.tile_pool(name="score_pool", bufs=3))
         tap_pool = ctx.enter_context(tc.tile_pool(name="tap_pool", bufs=2))
         weight_pool = ctx.enter_context(tc.tile_pool(name="weight_pool", bufs=3))
-        band_pool = ctx.enter_context(tc.tile_pool(name="band_pool", bufs=2))
         far_pool = ctx.enter_context(tc.tile_pool(name="far_pool", bufs=2))
         out_pool = ctx.enter_context(tc.tile_pool(name="out_pool", bufs=2))
 
-        x_of, grouped_of, code_of, q_of, vf_of, whole_of, gain_of = {}, {}, {}, {}, {}, {}, {}
+        grouped_of, code_of, qf_of, q_of, vf_of, whole_of, gain_of = {}, {}, {}, {}, {}, {}, {}
         q_ps_of, score_of, weight_of, skewed_of, band_of, far_of, near_of = {}, {}, {}, {}, {}, {}, {}
         scratch = out.rearrange("b n e -> (b n e)")
+
+        def load_gains(b):
+            for h in range(H):
+                nc.sync.dma_start(out=g_raw[:, b, h, :, :], in_=gains[b, h].rearrange("(t p) j -> p t j", p=P))
 
         def make_gain(c, tau):
             b, cc = divmod(c, NCC)
@@ -171,12 +182,6 @@ def tile_dwarfattention_pa_t_kernel(tc, x, W_qkv, b_qkv, gains, pos_bias, identi
             for h in range(H):
                 nc.scalar.activation(out=gain_of[c // GCH][:, :, TAP_AT[tau]:TAP_AT[tau] + NS, h],
                                      in_=g_raw[:, b, h, cc * TPC:cc * TPC + n, :], func=ACTF.Copy, scale=D4[tau])
-
-        def load_x(c):
-            b, cc = divmod(c, NCC)
-            x_of[c] = x_pool.tile([P, TPC, D], BF16, name="x_sb")
-            nc.sync.dma_start(out=x_of[c][:],
-                              in_=x[b, cc * CH:(cc + 1) * CH, :].rearrange("(t p) k -> p t k", p=P))
 
         def transpose_x(c, tl):
             if tl == 0:
@@ -212,17 +217,14 @@ def tile_dwarfattention_pa_t_kernel(tc, x, W_qkv, b_qkv, gains, pos_bias, identi
         def project_all(c):
             first = (c % NCC) * CH
             project(c, 1, k_f[:, KPAD + first:KPAD + first + CH])
-            q_f = q_pool.tile([P, CH], F32, name="q_f")
-            project(c, 0, q_f[:])
+            qf_of[c] = q_pool.tile([P, CH], F32, name="q_f")
+            project(c, 0, qf_of[c][:])
             vf_of[c] = vf_pool.tile([P, VPAD + CH], F32, name="v_f")
             if c % NCC == 0:
                 nc.gpsimd.memset(vf_of[c][:, 0:VPAD], 0.0)
             else:
                 nc.scalar.copy(out=vf_of[c][:, 0:VPAD], in_=vf_of[c - 1][:, CH:CH + VPAD])
             project(c, 2, vf_of[c][:, VPAD:VPAD + CH])
-            q_of[c] = q_pool.tile([P, TPC, E], F32, name="q_tok")
-            q_ps_of[c] = ps_q.tile([P, TPC, P], F32, name="q_ps")
-            token_major(q_f, 0, q_of[c][:], q_ps_of[c])
 
         def token_major(src, first, dst, tr=None):
             if tr is None:
@@ -232,8 +234,11 @@ def tile_dwarfattention_pa_t_kernel(tc, x, W_qkv, b_qkv, gains, pos_bias, identi
                                     identity=ident[:])
             nc.scalar.copy(out=dst, in_=tr[:])
 
-        def turn_kv(c):
+        def turn_qkv(c):
             t0 = (c % NCC) * TPC
+            q_of[c] = q_pool.tile([P, TPC, E], F32, name="q_tok")
+            q_ps_of[c] = ps_q.tile([P, TPC, P], F32, name="q_ps")
+            token_major(qf_of[c], 0, q_of[c][:], q_ps_of[c])
             token_major(k_f, KPAD + t0 * P, k_tok[:, t0:t0 + TPC, :])
             g0 = c * TPC
             token_major(vf_of[c], VPAD, v_tok[:, g0 % VRING:g0 % VRING + TPC, :])
@@ -381,6 +386,22 @@ def tile_dwarfattention_pa_t_kernel(tc, x, W_qkv, b_qkv, gains, pos_bias, identi
                     nc.gpsimd.tensor_tensor(out=far[:, dead:TPC, :], in0=far[:, dead:TPC, :],
                                             in1=part[:, dead:TPC, :], op=ALU.add)
 
+        def last_far_values(c):
+            far_of[c] = far_pool.tile([P, TPC, E], F32, name="far")
+            for s in FAR:
+                for tl in range(TPC):
+                    g = c * TPC + tl
+                    for h in range(H):
+                        hs = slice(h * HD, (h + 1) * HD)
+                        weight = weight_of[c][:, tl, s, h:h + 1]
+                        if s == FAR[0]:
+                            nc.vector.tensor_scalar_mul(out=far_of[c][:, tl, hs], in0=v_half[:, (g - 1) % BRING, hs],
+                                                        scalar1=weight)
+                        else:
+                            nc.vector.scalar_tensor_tensor(
+                                out=far_of[c][:, tl, hs], in0=v_tok[:, (g - OFFS[s] // P) % VRING, hs],
+                                scalar=weight, in1=far_of[c][:, tl, hs], op0=ALU.mult, op1=ALU.add)
+
         def near_values(c, h):
             cc = c % NCC
             hs = slice(h * HD, (h + 1) * HD)
@@ -407,12 +428,12 @@ def tile_dwarfattention_pa_t_kernel(tc, x, W_qkv, b_qkv, gains, pos_bias, identi
         def is_chunk(c):
             return 0 <= c < NCHUNK
 
-        load_x(0)
-        load_x(1)
         for c in range(-2, NCHUNK + 3):
             for step in range(TPC):
                 if step == 0 and is_chunk(c + 3) and c + 3 >= 2:
                     load_x(c + 3)
+                if step == 1 and c + 1 in (0, NCC):
+                    load_gains((c + 1) // NCC)
                 if is_chunk(c + 2):
                     transpose_x(c + 2, step)
                 if is_chunk(c + 1):
@@ -421,15 +442,19 @@ def tile_dwarfattention_pa_t_kernel(tc, x, W_qkv, b_qkv, gains, pos_bias, identi
                     if step == 1:
                         project_all(c + 1)
                     if step == 2:
-                        turn_kv(c + 1)
+                        turn_qkv(c + 1)
                 if is_chunk(c):
                     scores(c, step)
                 if c % GCH == 0 and is_chunk(c):
                     make_gain(c, step)
                 if step == 0 and is_chunk(c - 1):
-                    weights(c - 1)
-                    skew(c - 1)
-                    far_values(c - 1)
+                    with tc.high_priority():
+                        weights(c - 1)
+                        skew(c - 1)
+                    if c == NCHUNK:
+                        last_far_values(c - 1)
+                    else:
+                        far_values(c - 1)
                 if step == 3 and is_chunk(c - 1):
                     band(c - 1, 0)
                 if step == 0 and is_chunk(c - 2):
@@ -437,6 +462,7 @@ def tile_dwarfattention_pa_t_kernel(tc, x, W_qkv, b_qkv, gains, pos_bias, identi
                     near_values(c - 2, 0)
                 if step == 1 and is_chunk(c - 2):
                     near_values(c - 2, 1)
+                if step == 3 and is_chunk(c - 2):
                     finish(c - 2)
         for c in range(HOLD0, NCHUNK):
             b, cc = divmod(c, NCC)

@@ -29,25 +29,34 @@ NEAR = [s for s in RISING if OFFS[s] <= P]
 FAR = [s for s in RISING if OFFS[s] > P]
 WHOLE = [s for s in range(NOFF) if OFFS[s] % P == 0]
 CUT = [s for s in range(NOFF) if OFFS[s] % P != 0]
-NFEW = 6
+DENSE = [0] + CUT + [OFFS.index(P)]
+SPARSE = [s for s in WHOLE if s not in DENSE]
+NFEW = 2
+NG, NR = 16, 4
+NCOL = len(DENSE) * H
+NCUT = len(CUT) // 2
 TAP0, TAP1, TAP2, TAP3 = 1, 12, 24, 36
 NTAP = 47
 TAP_AT = (TAP0, TAP1, TAP2 + 1, TAP3)
-KPAD = P
 VPAD = 64
-GCH = 4
+GCH = 1
 ROW = 2 * P + 1
 UNIT = P * ROW
 VRING = 36
-BRING = 16
+BRING = 12
 SCR0 = B * N * E - H * TPC * UNIT
-HOLD0 = SCR0 // (CH * E)
+HOLD0 = NCC
+KPLACES = 3
 FLOPS = 2 * B * N * D * 3 * E + 4 * B * H * N * HD * NOFF
 
 
 def dead_tiles(cc, s):
     first = max(0, -((P - 1 - OFFS[s]) // P))
     return min(TPC, max(0, first - cc * TPC))
+
+
+def key_place(c):
+    return c if c < HOLD0 else HOLD0 + (c - HOLD0) % KPLACES
 
 
 def runs_of(places):
@@ -64,10 +73,9 @@ def tile_dwarfattention_pa_t_kernel(tc, x, W_qkv, b_qkv, gains, pos_bias, identi
     nc = tc.nc
     with ExitStack() as ctx:
         const = ctx.enter_context(tc.tile_pool(name="const", bufs=1))
-        ps_tr = ctx.enter_context(tc.psum_pool(name="ps_tr", bufs=2))
-        ps_mx = ctx.enter_context(tc.psum_pool(name="ps_mx", bufs=1))
-        ps_q = ctx.enter_context(tc.psum_pool(name="ps_q", bufs=1))
-        ps_cut = ctx.enter_context(tc.psum_pool(name="ps_cut", bufs=3))
+        ps_tr = ctx.enter_context(tc.psum_pool(name="ps_tr", bufs=3))
+        ps_q = ctx.enter_context(tc.psum_pool(name="ps_q", bufs=2))
+        ps_sum = ctx.enter_context(tc.psum_pool(name="ps_sum", bufs=2))
         ps_near = ctx.enter_context(tc.psum_pool(name="ps_near", bufs=1))
 
         ident = const.tile([P, P], F32, name="ident")
@@ -78,7 +86,6 @@ def tile_dwarfattention_pa_t_kernel(tc, x, W_qkv, b_qkv, gains, pos_bias, identi
         pb_bc = const.tile([P, NTAP, H], F32, name="pb_bc")
         g_raw = const.tile([P, B, H, NT, NS], BF16, name="g_raw")
         bypass = const.tile([P, H], F32, name="bypass")
-        k_f = const.tile([P, KPAD + N], F32, name="k_f")
         k_tok = const.tile([P, NT, E], F32, name="k_tok")
         v_tok = const.tile([P, VRING, E], F32, name="v_tok")
         v_half = const.tile([P, BRING, E], F32, name="v_half")
@@ -86,12 +93,11 @@ def tile_dwarfattention_pa_t_kernel(tc, x, W_qkv, b_qkv, gains, pos_bias, identi
         spare = const.tile([P, HD], F32, name="spare")
         rows = const.tile([P, H, TPC, ROW], F32, name="rows")
         nc.gpsimd.memset(rows[:], 0.0)
-        nc.gpsimd.memset(k_f[:, 0:KPAD], 0.0)
         nc.gpsimd.memset(pb_bc[:], 0.0)
 
         x_pool = ctx.enter_context(tc.tile_pool(name="x_pool", bufs=2))
-        grouped_pool = ctx.enter_context(tc.tile_pool(name="grouped_pool", bufs=2))
-        code_pool = ctx.enter_context(tc.tile_pool(name="code_pool", bufs=2))
+        grouped_pool = ctx.enter_context(tc.tile_pool(name="grouped_pool", bufs=1))
+        code_pool = ctx.enter_context(tc.tile_pool(name="code_pool", bufs=1))
         x_of = {}
 
         def load_x(c):
@@ -156,15 +162,18 @@ def tile_dwarfattention_pa_t_kernel(tc, x, W_qkv, b_qkv, gains, pos_bias, identi
         vf_pool = ctx.enter_context(tc.tile_pool(name="vf_pool", bufs=2))
         q_pool = ctx.enter_context(tc.tile_pool(name="q_pool", bufs=2))
         whole_pool = ctx.enter_context(tc.tile_pool(name="whole_pool", bufs=1))
-        cut_pool = ctx.enter_context(tc.tile_pool(name="cut_pool", bufs=3))
+        key_pool = ctx.enter_context(tc.tile_pool(name="key_pool", bufs=2))
+        prod_pool = ctx.enter_context(tc.tile_pool(name="prod_pool", bufs=3))
+        sum_pool = ctx.enter_context(tc.tile_pool(name="sum_pool", bufs=2))
         score_pool = ctx.enter_context(tc.tile_pool(name="score_pool", bufs=3))
         tap_pool = ctx.enter_context(tc.tile_pool(name="tap_pool", bufs=2))
         weight_pool = ctx.enter_context(tc.tile_pool(name="weight_pool", bufs=3))
         far_pool = ctx.enter_context(tc.tile_pool(name="far_pool", bufs=2))
         out_pool = ctx.enter_context(tc.tile_pool(name="out_pool", bufs=2))
 
-        grouped_of, code_of, qf_of, q_of, vf_of, whole_of, gain_of = {}, {}, {}, {}, {}, {}, {}
+        key_of, sum_of, grouped_of, code_of, kf_of, qf_of, vf_of, whole_of, gain_of = [{} for i in range(9)]
         q_ps_of, score_of, weight_of, skewed_of, band_of, far_of, near_of = {}, {}, {}, {}, {}, {}, {}
+        rows_of_out = out.rearrange("b n e -> (b n) e")
         scratch = out.rearrange("b n e -> (b n e)")
 
         def load_gains(b):
@@ -176,7 +185,7 @@ def tile_dwarfattention_pa_t_kernel(tc, x, W_qkv, b_qkv, gains, pos_bias, identi
             n = GCH * TPC
             if tau == 0:
                 gain_of[c // GCH] = gain_pool.tile([P, n, NTAP, H], F32, name="gain")
-                nc.gpsimd.memset(gain_of[c // GCH][:, :, TAP2 - 1:TAP2 + 1, :], 0.0)
+                nc.vector.memset(gain_of[c // GCH][:, :, TAP2 - 1:TAP2 + 1, :], 0.0)
                 nc.scalar.copy(out=gain_of[c // GCH][:, :, 0, :],
                                in_=bypass[:].unsqueeze(1).to_broadcast([P, n, H]))
             for h in range(H):
@@ -206,7 +215,7 @@ def tile_dwarfattention_pa_t_kernel(tc, x, W_qkv, b_qkv, gains, pos_bias, identi
 
         def project(c, f, dst):
             codes, scales = code_of[c]
-            acc = ps_mx.tile([P, CH], F32, name="acc", tag="mx")
+            acc = ps_tr.tile([P, CH], F32, name="acc", tag="tr")
             for g in range(2):
                 nc.tensor.matmul_mx(out=acc[:], lhsT=w_codes[:, g, f * P:(f + 1) * P].bitcast(FP8X4),
                                     lhsT_scale=w_scales[:, g, f * P:(f + 1) * P],
@@ -214,11 +223,15 @@ def tile_dwarfattention_pa_t_kernel(tc, x, W_qkv, b_qkv, gains, pos_bias, identi
                                     start=(g == 0), stop=(g == 1))
             nc.scalar.activation(out=dst, in_=acc[:], func=ACTF.Identity, bias=bias_col[:, f:f + 1], scale=1.0)
 
-        def project_all(c):
-            first = (c % NCC) * CH
-            project(c, 1, k_f[:, KPAD + first:KPAD + first + CH])
+        def project_k(c):
+            kf_of[c] = q_pool.tile([P, CH], F32, name="k_f")
+            project(c, 1, kf_of[c][:])
+
+        def project_q(c):
             qf_of[c] = q_pool.tile([P, CH], F32, name="q_f")
             project(c, 0, qf_of[c][:])
+
+        def project_v(c):
             vf_of[c] = vf_pool.tile([P, VPAD + CH], F32, name="v_f")
             if c % NCC == 0:
                 nc.gpsimd.memset(vf_of[c][:, 0:VPAD], 0.0)
@@ -226,74 +239,117 @@ def tile_dwarfattention_pa_t_kernel(tc, x, W_qkv, b_qkv, gains, pos_bias, identi
                 nc.scalar.copy(out=vf_of[c][:, 0:VPAD], in_=vf_of[c - 1][:, CH:CH + VPAD])
             project(c, 2, vf_of[c][:, VPAD:VPAD + CH])
 
-        def token_major(src, first, dst, tr=None):
-            if tr is None:
-                tr = ps_tr.tile([P, TPC, P], F32, name="tok_tr", tag="tr")
+        def turn(src, first, tr):
             for tl in range(TPC):
                 nc.tensor.transpose(out=tr[:, tl, :], in_=src[:, first + tl * P:first + (tl + 1) * P],
                                     identity=ident[:])
+
+        def token_major(src, first, dst):
+            tr = ps_tr.tile([P, TPC, P], F32, name="tok_tr", tag="tr")
+            turn(src, first, tr)
             nc.scalar.copy(out=dst, in_=tr[:])
 
-        def turn_qkv(c):
-            t0 = (c % NCC) * TPC
-            q_of[c] = q_pool.tile([P, TPC, E], F32, name="q_tok")
+        def turn_q(c):
             q_ps_of[c] = ps_q.tile([P, TPC, P], F32, name="q_ps")
-            token_major(qf_of[c], 0, q_of[c][:], q_ps_of[c])
-            token_major(k_f, KPAD + t0 * P, k_tok[:, t0:t0 + TPC, :])
-            g0 = c * TPC
-            token_major(vf_of[c], VPAD, v_tok[:, g0 % VRING:g0 % VRING + TPC, :])
-            token_major(vf_of[c], 0, v_half[:, g0 % BRING:g0 % BRING + TPC, :])
+            turn(qf_of[c], 0, q_ps_of[c])
 
-        def scores(c, tl):
+        def turn_k(c):
+            t0 = (c % NCC) * TPC
+            token_major(kf_of[c], 0, k_tok[:, t0:t0 + TPC, :])
+            row = key_place(c) * CH
+            nc.sync.dma_start(out=rows_of_out[row:row + CH, :].rearrange("(t p) e -> p t e", p=P),
+                              in_=k_tok[:, t0:t0 + TPC, :])
+
+        def load_keys(c, half):
+            for fam in range(2):
+                keys = key_pool.tile([P, NCUT, 2, E], F32, name="keys%d" % fam)
+                key_of[(c, half, fam)] = keys
+                for i in range(NCUT):
+                    o = OFFS[CUT[fam * NCUT + i]]
+                    row = key_place(c) * CH + half * 2 * P - o
+                    joined = c % NCC != 0 and key_place(c) == key_place(c - 1) + 1
+                    if half == 1 or joined:
+                        nc.sync.dma_start(out=keys[:, i, :, :],
+                                          in_=rows_of_out[row:row + 2 * P, :].rearrange("(t p) e -> p t e", p=P))
+                        continue
+                    for tl in range(2):
+                        early = min(P, max(0, o - tl * P))
+                        if early and c % NCC == 0:
+                            nc.vector.memset(keys[0:early, i, tl, :], 0.0)
+                        if early and c % NCC != 0:
+                            last = key_place(c - 1) * CH + CH + tl * P - o
+                            nc.sync.dma_start(out=keys[0:early, i, tl, :], in_=rows_of_out[last:last + early, :])
+                        if early < P:
+                            nc.sync.dma_start(out=keys[early:P, i, tl, :],
+                                              in_=rows_of_out[row + tl * P + early:row + (tl + 1) * P, :])
+
+        def turn_v(c, shift, ring, size):
+            g0 = (c * TPC) % size
+            token_major(vf_of[c], VPAD - shift, ring[:, g0:g0 + TPC, :])
+
+        def whole_products(c, i):
             cc = c % NCC
-            t0 = cc * TPC
-            if tl == 0:
-                score_of[c] = score_pool.tile([P, TPC, NOFF, H], F32, name="score")
-                whole_of[c] = whole_pool.tile([P, len(WHOLE), TPC, E], F32, name="whole")
-                if any(dead_tiles(cc, s) for s in range(NOFF)):
-                    nc.vector.memset(score_of[c][:], 0.0)
-            score, whole = score_of[c], whole_of[c]
-            q_t = q_of[c][:, tl, :]
-            places = [s for s in CUT if dead_tiles(cc, s) <= tl]
-            prod = cut_pool.tile([P, len(CUT), E], F32, name="prod")
-            for g in range(0, len(places), 4):
-                cut = ps_cut.tile([P, 4, P], F32, name="cut", tag="cut")
-                for i, s in enumerate(places[g:g + 4]):
-                    first = KPAD + (t0 + tl) * P - OFFS[s]
-                    nc.tensor.transpose(out=cut[:, i, :], in_=k_f[:, first:first + P], identity=ident[:])
-                n = len(places[g:g + 4])
-                nc.vector.tensor_tensor(out=prod[:, g:g + n, :], in0=cut[:, 0:n, :],
-                                        in1=q_t.unsqueeze(1).to_broadcast([P, n, E]), op=ALU.mult)
-            for i in range(tl, len(WHOLE), 2) if tl < 2 else ():
-                s = WHOLE[i]
-                dead = dead_tiles(cc, s)
-                if dead < TPC:
-                    first = t0 - OFFS[s] // P
-                    nc.vector.tensor_tensor(out=whole[:, i, dead:TPC, :], in0=k_tok[:, first + dead:first + TPC, :],
-                                            in1=q_ps_of[c][:, dead:TPC, :], op=ALU.mult)
-            for i, s in enumerate(places):
-                if s < NFEW:
+            dead = dead_tiles(cc, SPARSE[i])
+            if dead < TPC:
+                first = cc * TPC - OFFS[SPARSE[i]] // P
+                nc.vector.tensor_tensor(out=whole_of[c][:, i, dead:TPC, :], in0=k_tok[:, first + dead:first + TPC, :],
+                                        in1=q_ps_of[c][:, dead:TPC, :], op=ALU.mult)
+
+        def whole_sums(c):
+            cc = c % NCC
+            for i in range(NFEW):
+                for t in range(dead_tiles(cc, SPARSE[i]), TPC):
                     for h in range(H):
-                        nc.scalar.activation(out=spare[:], in_=prod[:, i, h * HD:(h + 1) * HD], func=ACTF.Copy,
-                                             accum_out=score[:, tl, s, h:h + 1])
-            for i, s, ln in runs_of(places):
-                skip = max(0, NFEW - s)
-                nc.vector.tensor_reduce(out=score[:, tl, s + skip:s + ln, :],
-                                        in_=prod[:, i + skip:i + ln, :].rearrange("p s (h d) -> p s h d", h=H),
+                        nc.scalar.activation(out=spare[:], in_=whole_of[c][:, i, t, h * HD:(h + 1) * HD],
+                                             func=ACTF.Copy, accum_out=score_of[c][:, t, SPARSE[i], h:h + 1])
+            for dead in range(TPC):
+                for j, s, ln in runs_of([s for s in SPARSE[NFEW:] if dead_tiles(cc, s) == dead]):
+                    i = SPARSE.index(s)
+                    nc.vector.tensor_reduce(
+                        out=score_of[c][:, dead:TPC, s:s + ln, :].rearrange("p t s h -> p s t h"),
+                        in_=whole_of[c][:, i:i + ln, dead:TPC, :].rearrange("p s t (h d) -> p s t h d", h=H),
+                        axis=AX.X, op=ALU.add)
+
+        def dense_products(c, tl):
+            t = (c % NCC) * TPC + tl
+            q_t = q_ps_of[c][:, tl, :]
+            prod = prod_pool.tile([P, NG, NCOL, NR], F32, name="prod")
+
+            def times_q(keys, i, n):
+                nc.vector.tensor_tensor(
+                    out=prod[:, :, i * H:(i + n) * H, :].rearrange("p g (s h) r -> p s h g r", h=H),
+                    in0=keys.rearrange("p s (h g r) -> p s h g r", h=H, g=NG),
+                    in1=q_t.rearrange("p (h g r) -> p h g r", h=H, g=NG).unsqueeze(1)
+                    .to_broadcast([P, n, H, NG, NR]), op=ALU.mult)
+
+            times_q(k_tok[:, t:t + 1, :], 0, 1)
+            for fam in range(2):
+                times_q(key_of[(c, tl // 2, fam)][:, :, tl % 2, :], 1 + fam * NCUT, NCUT)
+            if t > 0:
+                times_q(k_tok[:, t - 1:t, :], len(DENSE) - 1, 1)
+            else:
+                nc.vector.memset(prod[:, :, NCOL - H:NCOL, :], 0.0)
+            bank = ps_sum.tile([P, CH], F32, name="bank")
+            acc = bank[:, 0:P]
+            for i in range(NG):
+                nc.tensor.matmul(out=acc, lhsT=prod[:, i, :, :].rearrange("p k r -> p (k r)"), rhs=ident[:],
+                                 is_transpose=True, start=(i == 0), stop=(i == NG - 1))
+            nc.scalar.copy(out=sum_of[c][:, tl, :], in_=acc)
+
+        def dense_scores(c):
+            back = ps_tr.tile([P, TPC, P], F32, name="back", tag="tr")
+            turn(sum_of[c][:].rearrange("p t k -> p (t k)"), 0, back)
+            view = back[:].rearrange("p t (s h r) -> p t s h r", h=H, r=NR)
+            for i, s, ln in runs_of(DENSE):
+                nc.vector.tensor_reduce(out=score_of[c][:, :, s:s + ln, :], in_=view[:, :, i:i + ln, :, :],
                                         axis=AX.X, op=ALU.add)
-            if tl == 2:
-                for t in range(TPC):
-                    for h in range(H):
-                        nc.scalar.activation(out=spare[:], in_=whole[:, 0, t, h * HD:(h + 1) * HD], func=ACTF.Copy,
-                                             accum_out=score[:, t, 0, h:h + 1])
-                for dead in range(TPC):
-                    live = [s for s in WHOLE if s >= NFEW and dead_tiles(cc, s) == dead]
-                    for j, s, ln in runs_of(live):
-                        i = WHOLE.index(s)
-                        nc.vector.tensor_reduce(
-                            out=score[:, dead:TPC, s:s + ln, :].rearrange("p t s h -> p s t h"),
-                            in_=whole[:, i:i + ln, dead:TPC, :].rearrange("p s t (h d) -> p s t h d", h=H),
-                            axis=AX.X, op=ALU.add)
+
+        def open_scores(c):
+            score_of[c] = score_pool.tile([P, TPC, NOFF, H], F32, name="score")
+            whole_of[c] = whole_pool.tile([P, len(SPARSE), TPC, E], F32, name="whole")
+            sum_of[c] = sum_pool.tile([P, TPC, P], F32, name="sum")
+            if any(dead_tiles(c % NCC, s) for s in SPARSE):
+                nc.vector.memset(score_of[c][:], 0.0)
 
         def weights(c):
             score = score_of[c]
@@ -339,21 +395,21 @@ def tile_dwarfattention_pa_t_kernel(tc, x, W_qkv, b_qkv, gains, pos_bias, identi
                 nc.scalar.copy(out=rows[:, :, :, P - OFFS[s]], in_=w[:, :, s, :].rearrange("p t h -> p h t"))
             for h in range(H):
                 area = scratch[SCR0 + h * TPC * UNIT:SCR0 + (h + 1) * TPC * UNIT]
-                nc.sync.dma_start(out=area.rearrange("(t p w) -> p t w", t=TPC, p=P), in_=rows[:, h, :, :])
+                nc.scalar.dma_start(out=area.rearrange("(t p w) -> p t w", t=TPC, p=P), in_=rows[:, h, :, :])
                 skewed_of[(c, h)] = band_pool.tile([P, TPC, 2 * P], F32, name="skewed")
                 nc.sync.dma_start(out=skewed_of[(c, h)][:],
                                   in_=area.rearrange("(t r) -> t r", t=TPC)[:, 0:2 * P * P]
                                   .rearrange("t (p m) -> p t m", p=P))
 
-        def band(c, h):
-            band_of[(c, h)] = band_pool.tile([P, 2 * TPC, P], F32, name="band")
-            for half in range(2):
-                tr = ps_tr.tile([P, 4, P], F32, name="band_tr", tag="tr")
-                for i in range(4):
-                    tl, kb = divmod(4 * half + i, 2)
-                    nc.tensor.transpose(out=tr[:, i, :], in_=skewed_of[(c, h)][:, tl, kb * P:(kb + 1) * P],
-                                        identity=ident[:])
-                nc.scalar.copy(out=band_of[(c, h)][:, 4 * half:4 * half + 4, :], in_=tr[:])
+        def band(c, h, half):
+            if half == 0:
+                band_of[(c, h)] = band_pool.tile([P, 2 * TPC, P], F32, name="band")
+            tr = ps_tr.tile([P, 4, P], F32, name="band_tr", tag="tr")
+            for i in range(4):
+                tl, kb = divmod(4 * half + i, 2)
+                nc.tensor.transpose(out=tr[:, i, :], in_=skewed_of[(c, h)][:, tl, kb * P:(kb + 1) * P],
+                                    identity=ident[:])
+            nc.scalar.copy(out=band_of[(c, h)][:, 4 * half:4 * half + 4, :], in_=tr[:])
 
         def ring_pieces(first, n, size):
             at = first % size
@@ -402,17 +458,16 @@ def tile_dwarfattention_pa_t_kernel(tc, x, W_qkv, b_qkv, gains, pos_bias, identi
                                 out=far_of[c][:, tl, hs], in0=v_tok[:, (g - OFFS[s] // P) % VRING, hs],
                                 scalar=weight, in1=far_of[c][:, tl, hs], op0=ALU.mult, op1=ALU.add)
 
-        def near_values(c, h):
+        def near_values(c, h, tl):
             cc = c % NCC
             hs = slice(h * HD, (h + 1) * HD)
-            if h == 0:
+            if h == 0 and tl == 0:
                 near_of[c] = ps_near.tile([P, TPC, E], F32, name="near")
-            for tl in range(TPC):
-                blocks = [kb for kb in range(2) if cc * TPC + tl - 1 + kb >= 0]
-                for kb in blocks:
-                    nc.tensor.matmul(out=near_of[c][:, tl, hs], lhsT=band_of[(c, h)][:, 2 * tl + kb, :],
-                                     rhs=v_tok[:, (c * TPC + tl - 1 + kb) % VRING, hs],
-                                     start=(kb == blocks[0]), stop=(kb == 1))
+            blocks = [kb for kb in range(2) if cc * TPC + tl - 1 + kb >= 0]
+            for kb in blocks:
+                nc.tensor.matmul(out=near_of[c][:, tl, hs], lhsT=band_of[(c, h)][:, 2 * tl + kb, :],
+                                 rhs=v_tok[:, (c * TPC + tl - 1 + kb) % VRING, hs],
+                                 start=(kb == blocks[0]), stop=(kb == 1))
 
         def finish(c):
             b, cc = divmod(c, NCC)
@@ -428,42 +483,67 @@ def tile_dwarfattention_pa_t_kernel(tc, x, W_qkv, b_qkv, gains, pos_bias, identi
         def is_chunk(c):
             return 0 <= c < NCHUNK
 
-        for c in range(-2, NCHUNK + 3):
-            for step in range(TPC):
-                if step == 0 and is_chunk(c + 3) and c + 3 >= 2:
+        def work(c, slot):
+            if slot == 0:
+                if is_chunk(c + 3) and c + 3 >= 2:
                     load_x(c + 3)
-                if step == 1 and c + 1 in (0, NCC):
-                    load_gains((c + 1) // NCC)
-                if is_chunk(c + 2):
-                    transpose_x(c + 2, step)
                 if is_chunk(c + 1):
-                    if step == 0:
-                        quantise_x(c + 1)
-                    if step == 1:
-                        project_all(c + 1)
-                    if step == 2:
-                        turn_qkv(c + 1)
-                if is_chunk(c):
-                    scores(c, step)
-                if c % GCH == 0 and is_chunk(c):
-                    make_gain(c, step)
-                if step == 0 and is_chunk(c - 1):
+                    quantise_x(c + 1)
+            if slot == 4 and c + 1 in (0, NCC):
+                load_gains((c + 1) // NCC)
+            if slot % 4 == 1 and is_chunk(c + 2):
+                transpose_x(c + 2, slot // 4)
+            if is_chunk(c + 1):
+                if slot == 2:
+                    project_k(c + 1)
+                if slot == 3:
+                    project_q(c + 1)
+                if slot == 4:
+                    project_v(c + 1)
+                if slot == 6:
+                    turn_k(c + 1)
+                if slot == 7:
+                    load_keys(c + 1, 0)
+                if slot == 8:
+                    turn_v(c + 1, 0, v_tok, VRING)
+                if slot == 10:
+                    turn_v(c + 1, VPAD, v_half, BRING)
+                if slot == 11:
+                    turn_q(c + 1)
+            if is_chunk(c):
+                if slot == 0:
+                    open_scores(c)
+                    load_keys(c, 1)
+                if slot < len(SPARSE):
+                    whole_products(c, slot)
+                if slot == len(SPARSE):
+                    whole_sums(c)
+                if slot % TPC == 0:
+                    dense_products(c, slot // TPC)
+            if is_chunk(c) and c % GCH == 0 and slot % 4 == 3:
+                make_gain(c, slot // 4)
+            if is_chunk(c - 1):
+                if slot == 2:
                     with tc.high_priority():
+                        dense_scores(c - 1)
                         weights(c - 1)
                         skew(c - 1)
                     if c == NCHUNK:
                         last_far_values(c - 1)
                     else:
                         far_values(c - 1)
-                if step == 3 and is_chunk(c - 1):
-                    band(c - 1, 0)
-                if step == 0 and is_chunk(c - 2):
-                    band(c - 2, 1)
-                    near_values(c - 2, 0)
-                if step == 1 and is_chunk(c - 2):
-                    near_values(c - 2, 1)
-                if step == 3 and is_chunk(c - 2):
+            if is_chunk(c - 2):
+                if slot < 2 * H:
+                    band(c - 2, slot // 2, slot % 2)
+                if slot in (5, 9):
+                    for tl in range(TPC):
+                        near_values(c - 2, (slot - 5) // TPC, tl)
+                if slot == 14:
                     finish(c - 2)
+
+        for c in range(-2, NCHUNK + 3):
+            for slot in range(4 * TPC):
+                work(c, slot)
         for c in range(HOLD0, NCHUNK):
             b, cc = divmod(c, NCC)
             nc.sync.dma_start(out=out[b, cc * CH:(cc + 1) * CH, :].rearrange("(t p) e -> p t e", p=P),

@@ -28,19 +28,20 @@ RISING = sorted(range(NOFF), key=lambda s: OFFS[s])
 NEAR = [s for s in RISING if OFFS[s] <= P]
 FAR = [s for s in RISING if OFFS[s] > P]
 WHOLE = [s for s in range(NOFF) if OFFS[s] % P == 0]
-CUT = [s for s in range(NOFF) if OFFS[s] % P != 0]
-DENSE = [0] + CUT + [OFFS.index(P)]
+CUT = [s for s in range(1, 1 + NPOW) if OFFS[s] % P != 0]
+MOVED = [s for s in range(1 + NPOW, NOFF) if OFFS[s] % P != 0]
+DENSE = MOVED + [OFFS.index(P)]
 SPARSE = [s for s in WHOLE if s not in DENSE]
-NFEW = 2
-NG, NR = 16, 4
+NFEW = 4
+NG, NR = 8, 8
 NCOL = len(DENSE) * H
-NCUT = len(CUT) // 2
+KPAD = 64
 TAP0, TAP1, TAP2, TAP3 = 1, 12, 24, 36
 NTAP = 47
 TAP_AT = (TAP0, TAP1, TAP2 + 1, TAP3)
 VPAD = 64
 GCH = 1
-ROW = 2 * P + 1
+ROW = 2 * P + 8
 UNIT = P * ROW
 VRING = 36
 BRING = 12
@@ -73,8 +74,9 @@ def tile_dwarfattention_pa_t_kernel(tc, x, W_qkv, b_qkv, gains, pos_bias, identi
     nc = tc.nc
     with ExitStack() as ctx:
         const = ctx.enter_context(tc.tile_pool(name="const", bufs=1))
-        ps_tr = ctx.enter_context(tc.psum_pool(name="ps_tr", bufs=3))
-        ps_q = ctx.enter_context(tc.psum_pool(name="ps_q", bufs=2))
+        ps_tr = ctx.enter_context(tc.psum_pool(name="ps_tr", bufs=2))
+        ps_q = ctx.enter_context(tc.psum_pool(name="ps_q", bufs=1))
+        ps_cut = ctx.enter_context(tc.psum_pool(name="ps_cut", bufs=2))
         ps_sum = ctx.enter_context(tc.psum_pool(name="ps_sum", bufs=2))
         ps_near = ctx.enter_context(tc.psum_pool(name="ps_near", bufs=1))
 
@@ -162,7 +164,8 @@ def tile_dwarfattention_pa_t_kernel(tc, x, W_qkv, b_qkv, gains, pos_bias, identi
         vf_pool = ctx.enter_context(tc.tile_pool(name="vf_pool", bufs=2))
         q_pool = ctx.enter_context(tc.tile_pool(name="q_pool", bufs=2))
         whole_pool = ctx.enter_context(tc.tile_pool(name="whole_pool", bufs=1))
-        key_pool = ctx.enter_context(tc.tile_pool(name="key_pool", bufs=2))
+        key_pool = ctx.enter_context(tc.tile_pool(name="key_pool", bufs=3))
+        cut_pool = ctx.enter_context(tc.tile_pool(name="cut_pool", bufs=3))
         prod_pool = ctx.enter_context(tc.tile_pool(name="prod_pool", bufs=3))
         sum_pool = ctx.enter_context(tc.tile_pool(name="sum_pool", bufs=2))
         score_pool = ctx.enter_context(tc.tile_pool(name="score_pool", bufs=3))
@@ -171,8 +174,8 @@ def tile_dwarfattention_pa_t_kernel(tc, x, W_qkv, b_qkv, gains, pos_bias, identi
         far_pool = ctx.enter_context(tc.tile_pool(name="far_pool", bufs=2))
         out_pool = ctx.enter_context(tc.tile_pool(name="out_pool", bufs=2))
 
-        key_of, sum_of, grouped_of, code_of, kf_of, qf_of, vf_of, whole_of, gain_of = [{} for i in range(9)]
-        q_ps_of, score_of, weight_of, skewed_of, band_of, far_of, near_of = {}, {}, {}, {}, {}, {}, {}
+        key_of, sum_of, grouped_of, code_of, kf_of, qf_of, q_of, vf_of, whole_of, gain_of = [{} for i in range(10)]
+        cut_of, q_ps_of, score_of, weight_of, skewed_of, band_of, far_of, near_of = {}, {}, {}, {}, {}, {}, {}, {}
         rows_of_out = out.rearrange("b n e -> (b n) e")
         scratch = out.rearrange("b n e -> (b n e)")
 
@@ -224,8 +227,12 @@ def tile_dwarfattention_pa_t_kernel(tc, x, W_qkv, b_qkv, gains, pos_bias, identi
             nc.scalar.activation(out=dst, in_=acc[:], func=ACTF.Identity, bias=bias_col[:, f:f + 1], scale=1.0)
 
         def project_k(c):
-            kf_of[c] = q_pool.tile([P, CH], F32, name="k_f")
-            project(c, 1, kf_of[c][:])
+            kf_of[c] = vf_pool.tile([P, KPAD + CH], F32, name="k_f")
+            if c % NCC == 0:
+                nc.vector.memset(kf_of[c][:, 0:KPAD], 0.0)
+            else:
+                nc.scalar.copy(out=kf_of[c][:, 0:KPAD], in_=kf_of[c - 1][:, CH:CH + KPAD])
+            project(c, 1, kf_of[c][:, KPAD:KPAD + CH])
 
         def project_q(c):
             qf_of[c] = q_pool.tile([P, CH], F32, name="q_f")
@@ -234,7 +241,7 @@ def tile_dwarfattention_pa_t_kernel(tc, x, W_qkv, b_qkv, gains, pos_bias, identi
         def project_v(c):
             vf_of[c] = vf_pool.tile([P, VPAD + CH], F32, name="v_f")
             if c % NCC == 0:
-                nc.gpsimd.memset(vf_of[c][:, 0:VPAD], 0.0)
+                nc.vector.memset(vf_of[c][:, 0:VPAD], 0.0)
             else:
                 nc.scalar.copy(out=vf_of[c][:, 0:VPAD], in_=vf_of[c - 1][:, CH:CH + VPAD])
             project(c, 2, vf_of[c][:, VPAD:VPAD + CH])
@@ -252,36 +259,37 @@ def tile_dwarfattention_pa_t_kernel(tc, x, W_qkv, b_qkv, gains, pos_bias, identi
         def turn_q(c):
             q_ps_of[c] = ps_q.tile([P, TPC, P], F32, name="q_ps")
             turn(qf_of[c], 0, q_ps_of[c])
+            q_of[c] = q_pool.tile([P, TPC, E], F32, name="q_tok")
+            nc.scalar.copy(out=q_of[c][:], in_=q_ps_of[c][:])
 
         def turn_k(c):
             t0 = (c % NCC) * TPC
-            token_major(kf_of[c], 0, k_tok[:, t0:t0 + TPC, :])
+            token_major(kf_of[c], KPAD, k_tok[:, t0:t0 + TPC, :])
             row = key_place(c) * CH
             nc.sync.dma_start(out=rows_of_out[row:row + CH, :].rearrange("(t p) e -> p t e", p=P),
                               in_=k_tok[:, t0:t0 + TPC, :])
 
         def load_keys(c, half):
-            for fam in range(2):
-                keys = key_pool.tile([P, NCUT, 2, E], F32, name="keys%d" % fam)
-                key_of[(c, half, fam)] = keys
-                for i in range(NCUT):
-                    o = OFFS[CUT[fam * NCUT + i]]
-                    row = key_place(c) * CH + half * 2 * P - o
-                    joined = c % NCC != 0 and key_place(c) == key_place(c - 1) + 1
-                    if half == 1 or joined:
-                        nc.sync.dma_start(out=keys[:, i, :, :],
-                                          in_=rows_of_out[row:row + 2 * P, :].rearrange("(t p) e -> p t e", p=P))
-                        continue
-                    for tl in range(2):
-                        early = min(P, max(0, o - tl * P))
-                        if early and c % NCC == 0:
-                            nc.vector.memset(keys[0:early, i, tl, :], 0.0)
-                        if early and c % NCC != 0:
-                            last = key_place(c - 1) * CH + CH + tl * P - o
-                            nc.sync.dma_start(out=keys[0:early, i, tl, :], in_=rows_of_out[last:last + early, :])
-                        if early < P:
-                            nc.sync.dma_start(out=keys[early:P, i, tl, :],
-                                              in_=rows_of_out[row + tl * P + early:row + (tl + 1) * P, :])
+            keys = key_pool.tile([P, len(MOVED), 2, E], F32, name="keys")
+            key_of[(c, half)] = keys
+            for i, s in enumerate(MOVED):
+                o = OFFS[s]
+                row = key_place(c) * CH + half * 2 * P - o
+                joined = c % NCC != 0 and key_place(c) == key_place(c - 1) + 1
+                if half == 1 or joined:
+                    nc.sync.dma_start(out=keys[:, i, :, :],
+                                      in_=rows_of_out[row:row + 2 * P, :].rearrange("(t p) e -> p t e", p=P))
+                    continue
+                for tl in range(2):
+                    early = min(P, max(0, o - tl * P))
+                    if early and c % NCC == 0:
+                        nc.vector.memset(keys[0:early, i, tl, :], 0.0)
+                    if early and c % NCC != 0:
+                        last = key_place(c - 1) * CH + CH + tl * P - o
+                        nc.sync.dma_start(out=keys[0:early, i, tl, :], in_=rows_of_out[last:last + early, :])
+                    if early < P:
+                        nc.sync.dma_start(out=keys[early:P, i, tl, :],
+                                          in_=rows_of_out[row + tl * P + early:row + (tl + 1) * P, :])
 
         def turn_v(c, shift, ring, size):
             g0 = (c * TPC) % size
@@ -295,20 +303,43 @@ def tile_dwarfattention_pa_t_kernel(tc, x, W_qkv, b_qkv, gains, pos_bias, identi
                 nc.vector.tensor_tensor(out=whole_of[c][:, i, dead:TPC, :], in0=k_tok[:, first + dead:first + TPC, :],
                                         in1=q_ps_of[c][:, dead:TPC, :], op=ALU.mult)
 
+        def few_sums(prods, score):
+            for h in range(H):
+                nc.scalar.activation(out=spare[:], in_=prods[:, h * HD:(h + 1) * HD], func=ACTF.Copy,
+                                     accum_out=score[:, h:h + 1])
+
         def whole_sums(c):
             cc = c % NCC
-            for i in range(NFEW):
-                for t in range(dead_tiles(cc, SPARSE[i]), TPC):
-                    for h in range(H):
-                        nc.scalar.activation(out=spare[:], in_=whole_of[c][:, i, t, h * HD:(h + 1) * HD],
-                                             func=ACTF.Copy, accum_out=score_of[c][:, t, SPARSE[i], h:h + 1])
+            for t in range(TPC):
+                few_sums(whole_of[c][:, 0, t, :], score_of[c][:, t, 0, :])
             for dead in range(TPC):
-                for j, s, ln in runs_of([s for s in SPARSE[NFEW:] if dead_tiles(cc, s) == dead]):
+                for j, s, ln in runs_of([s for s in SPARSE if s >= NFEW and dead_tiles(cc, s) == dead]):
                     i = SPARSE.index(s)
                     nc.vector.tensor_reduce(
                         out=score_of[c][:, dead:TPC, s:s + ln, :].rearrange("p t s h -> p s t h"),
                         in_=whole_of[c][:, i:i + ln, dead:TPC, :].rearrange("p s t (h d) -> p s t h d", h=H),
                         axis=AX.X, op=ALU.add)
+
+        def cut_products(c, tl, part):
+            if part == 0:
+                cut_of[(c, tl)] = cut_pool.tile([P, len(CUT), E], F32, name="cut_prod")
+            i0 = 4 * part
+            n = len(CUT[i0:i0 + 4])
+            cut = ps_cut.tile([P, 4, P], F32, name="cut")
+            for j in range(n):
+                first = KPAD + tl * P - OFFS[CUT[i0 + j]]
+                nc.tensor.transpose(out=cut[:, j, :], in_=kf_of[c][:, first:first + P], identity=ident[:])
+            nc.vector.tensor_tensor(out=cut_of[(c, tl)][:, i0:i0 + n, :], in0=cut[:, 0:n, :],
+                                    in1=q_of[c][:, tl, :].unsqueeze(1).to_broadcast([P, n, E]), op=ALU.mult)
+
+        def cut_sums(c, tl):
+            prod = cut_of[(c, tl)]
+            i = CUT.index(NFEW)
+            for j in range(i):
+                few_sums(prod[:, j, :], score_of[c][:, tl, CUT[j], :])
+            nc.vector.tensor_reduce(out=score_of[c][:, tl, NFEW:CUT[-1] + 1, :],
+                                    in_=prod[:, i:len(CUT), :].rearrange("p s (h d) -> p s h d", h=H),
+                                    axis=AX.X, op=ALU.add)
 
         def dense_products(c, tl):
             t = (c % NCC) * TPC + tl
@@ -322,9 +353,7 @@ def tile_dwarfattention_pa_t_kernel(tc, x, W_qkv, b_qkv, gains, pos_bias, identi
                     in1=q_t.rearrange("p (h g r) -> p h g r", h=H, g=NG).unsqueeze(1)
                     .to_broadcast([P, n, H, NG, NR]), op=ALU.mult)
 
-            times_q(k_tok[:, t:t + 1, :], 0, 1)
-            for fam in range(2):
-                times_q(key_of[(c, tl // 2, fam)][:, :, tl % 2, :], 1 + fam * NCUT, NCUT)
+            times_q(key_of[(c, tl // 2)][:, :, tl % 2, :], 0, len(MOVED))
             if t > 0:
                 times_q(k_tok[:, t - 1:t, :], len(DENSE) - 1, 1)
             else:
@@ -398,8 +427,8 @@ def tile_dwarfattention_pa_t_kernel(tc, x, W_qkv, b_qkv, gains, pos_bias, identi
                 nc.scalar.dma_start(out=area.rearrange("(t p w) -> p t w", t=TPC, p=P), in_=rows[:, h, :, :])
                 skewed_of[(c, h)] = band_pool.tile([P, TPC, 2 * P], F32, name="skewed")
                 nc.sync.dma_start(out=skewed_of[(c, h)][:],
-                                  in_=area.rearrange("(t r) -> t r", t=TPC)[:, 0:2 * P * P]
-                                  .rearrange("t (p m) -> p t m", p=P))
+                                  in_=area.rearrange("(t r) -> t r", t=TPC)[:, 0:P * (ROW - 1)]
+                                  .rearrange("t (p m) -> p t m", p=P)[:, :, 0:2 * P])
 
         def band(c, h, half):
             if half == 0:
@@ -489,7 +518,7 @@ def tile_dwarfattention_pa_t_kernel(tc, x, W_qkv, b_qkv, gains, pos_bias, identi
                     load_x(c + 3)
                 if is_chunk(c + 1):
                     quantise_x(c + 1)
-            if slot == 4 and c + 1 in (0, NCC):
+            if slot == 8 and c + 1 in (0, NCC):
                 load_gains((c + 1) // NCC)
             if slot % 4 == 1 and is_chunk(c + 2):
                 transpose_x(c + 2, slot // 4)
@@ -502,24 +531,28 @@ def tile_dwarfattention_pa_t_kernel(tc, x, W_qkv, b_qkv, gains, pos_bias, identi
                     project_v(c + 1)
                 if slot == 6:
                     turn_k(c + 1)
-                if slot == 7:
-                    load_keys(c + 1, 0)
+                if slot in (7, 9):
+                    load_keys(c + 1, (slot - 7) // 2)
                 if slot == 8:
                     turn_v(c + 1, 0, v_tok, VRING)
                 if slot == 10:
                     turn_v(c + 1, VPAD, v_half, BRING)
-                if slot == 11:
+                if slot == 13:
                     turn_q(c + 1)
             if is_chunk(c):
                 if slot == 0:
                     open_scores(c)
-                    load_keys(c, 1)
                 if slot < len(SPARSE):
                     whole_products(c, slot)
                 if slot == len(SPARSE):
                     whole_sums(c)
-                if slot % TPC == 0:
-                    dense_products(c, slot // TPC)
+                tl, part = divmod(slot, 4)
+                if part == 0:
+                    dense_products(c, tl)
+                if part in (1, 2):
+                    cut_products(c, tl, part - 1)
+                if part == 3:
+                    cut_sums(c, tl)
             if is_chunk(c) and c % GCH == 0 and slot % 4 == 3:
                 make_gain(c, slot // 4)
             if is_chunk(c - 1):
@@ -541,9 +574,13 @@ def tile_dwarfattention_pa_t_kernel(tc, x, W_qkv, b_qkv, gains, pos_bias, identi
                 if slot == 14:
                     finish(c - 2)
 
-        for c in range(-2, NCHUNK + 3):
+        for c in range(-2, NCHUNK):
             for slot in range(4 * TPC):
                 work(c, slot)
+        with tc.manual_schedule():
+            for c in range(NCHUNK, NCHUNK + 2):
+                for slot in range(4 * TPC):
+                    work(c, slot)
         for c in range(HOLD0, NCHUNK):
             b, cc = divmod(c, NCC)
             nc.sync.dma_start(out=out[b, cc * CH:(cc + 1) * CH, :].rearrange("(t p) e -> p t e", p=P),

@@ -26,7 +26,7 @@ OFFS = (0,) + tuple(1 << i for i in range(NPOW)) + tuple(3 << j for j in range(N
 NOFF = len(OFFS)
 RISING = sorted(range(NOFF), key=lambda s: OFFS[s])
 NEAR = [s for s in RISING if OFFS[s] <= P]
-FAR = [s for s in RISING if OFFS[s] > P]
+FAR = [s for s in range(NOFF) if OFFS[s] > P]
 WHOLE = [s for s in range(NOFF) if OFFS[s] % P == 0]
 CUT = [s for s in range(1, 1 + NPOW) if OFFS[s] % P != 0]
 MOVED = [s for s in range(1 + NPOW, NOFF) if OFFS[s] % P != 0]
@@ -39,14 +39,15 @@ KPAD = 64
 TAP0, TAP1, TAP2, TAP3 = 1, 12, 24, 36
 NTAP = 47
 TAP_AT = (TAP0, TAP1, TAP2 + 1, TAP3)
-VPAD = 64
+SHIFT = 64
+G_BANK = 8
 GCH = 1
 ROW = 2 * P + 8
 UNIT = P * ROW
 VRING = 36
 BRING = 12
 SCR0 = B * N * E - H * TPC * UNIT
-HOLD0 = NCC
+HOLD0 = NCC - 2
 KPLACES = 3
 FLOPS = 2 * B * N * D * 3 * E + 4 * B * H * N * HD * NOFF
 
@@ -58,6 +59,10 @@ def dead_tiles(cc, s):
 
 def key_place(c):
     return c if c < HOLD0 else HOLD0 + (c - HOLD0) % KPLACES
+
+
+def value_place(c):
+    return HOLD0 + KPLACES + c % 2
 
 
 def runs_of(places):
@@ -82,6 +87,8 @@ def tile_dwarfattention_pa_t_kernel(tc, x, W_qkv, b_qkv, gains, pos_bias, identi
 
         ident = const.tile([P, P], F32, name="ident")
         make_identity(nc, ident[:])
+        ident_bf = const.tile([P, P], BF16, name="ident_bf")
+        make_identity(nc, ident_bf[:])
         w_codes = const.tile([P, 2, 3 * P], U32, name="w_codes", align_bytes=64)
         w_scales = const.tile([P, 2, 3 * P], U8, name="w_scales", align_bytes=64)
         bias_col = const.tile([P, 4], F32, name="bias_col")
@@ -94,6 +101,7 @@ def tile_dwarfattention_pa_t_kernel(tc, x, W_qkv, b_qkv, gains, pos_bias, identi
         held = const.tile([P, (NCHUNK - HOLD0) * TPC, E], F32, name="held")
         spare = const.tile([P, HD], F32, name="spare")
         rows = const.tile([P, H, TPC, ROW], F32, name="rows")
+        g_rows = const.tile([P, P, NS], BF16, name="g_rows")
         nc.gpsimd.memset(rows[:], 0.0)
         nc.gpsimd.memset(pb_bc[:], 0.0)
 
@@ -105,10 +113,14 @@ def tile_dwarfattention_pa_t_kernel(tc, x, W_qkv, b_qkv, gains, pos_bias, identi
         def load_x(c):
             b, cc = divmod(c, NCC)
             x_of[c] = x_pool.tile([P, TPC, D], BF16, name="x_sb")
-            nc.sync.dma_start(out=x_of[c][:],
-                              in_=x[b, cc * CH:(cc + 1) * CH, :].rearrange("(t p) k -> p t k", p=P))
+            rows_of_x = x[b, cc * CH:(cc + 1) * CH, :].rearrange("(t p) k -> p t k", p=P)
+            step = 1 if c == 0 else TPC
+            for t in range(0, TPC, step):
+                nc.sync.dma_start(out=x_of[c][:, t:t + step, :], in_=rows_of_x[:, t:t + step, :])
 
         with tc.manual_schedule(), tc.tile_pool(name="setup", bufs=1) as setup:
+            ib_raw = setup.tile([P, H], BF16, name="ib_raw")
+            nc.sync.dma_start(out=ib_raw[:], in_=identity_bypass.partition_broadcast(P))
             b_rows = setup.tile([P, P], BF16, name="b_rows")
             nc.vector.memset(b_rows[:], 0.0)
             nc.sync.dma_start(out=b_rows[0:3, :], in_=b_qkv.rearrange("(f c) -> f c", c=P))
@@ -117,9 +129,18 @@ def tile_dwarfattention_pa_t_kernel(tc, x, W_qkv, b_qkv, gains, pos_bias, identi
             load_x(0)
             pb_raw = setup.tile([P, 4 * NS * H], BF16, name="pb_raw")
             nc.sync.dma_start(out=pb_raw[:], in_=pos_bias.rearrange("r h -> (r h)").partition_broadcast(P))
-            ib_raw = setup.tile([P, H], BF16, name="ib_raw")
-            nc.sync.dma_start(out=ib_raw[:], in_=identity_bypass.partition_broadcast(P))
             load_x(1)
+            nc.sync.dma_start(out=g_rows[:], in_=gains.rearrange("b h (t p) j -> (b h t) p j", p=P))
+
+            ib = setup.tile([P, H], F32, name="ib")
+            nc.vector.tensor_copy(out=ib[:], in_=ib_raw[:])
+            ib_e = setup.tile([P, H], F32, name="ib_e")
+            nc.scalar.activation(out=ib_e[:], in_=ib[:], func=ACTF.Abs)
+            nc.scalar.activation(out=ib_e[:], in_=ib_e[:], func=ACTF.Exp, scale=-1.0)
+            nc.vector.tensor_scalar_add(out=ib_e[:], in0=ib_e[:], scalar1=1.0)
+            nc.scalar.activation(out=ib_e[:], in_=ib_e[:], func=ACTF.Ln)
+            nc.vector.scalar_tensor_tensor(out=bypass[:], in0=ib[:], scalar=0.0, in1=ib_e[:],
+                                           op0=ALU.max, op1=ALU.add)
 
             w_grouped = setup.tile([P, 2, 3 * P, 2], F32, name="w_grouped", align_bytes=64)
             for f in range(3):
@@ -148,17 +169,6 @@ def tile_dwarfattention_pa_t_kernel(tc, x, W_qkv, b_qkv, gains, pos_bias, identi
             for tau in range(4):
                 nc.vector.tensor_copy(out=pb_bc[:, TAP_AT[tau]:TAP_AT[tau] + NS, :], in_=pb_view[:, tau, :, :])
 
-            ib = setup.tile([P, H], F32, name="ib")
-            nc.vector.tensor_copy(out=ib[:], in_=ib_raw[:])
-            ib_e = setup.tile([P, H], F32, name="ib_e")
-            nc.scalar.activation(out=ib_e[:], in_=ib[:], func=ACTF.Abs)
-            nc.scalar.activation(out=ib_e[:], in_=ib_e[:], func=ACTF.Exp, scale=-1.0)
-            nc.vector.tensor_scalar_add(out=ib_e[:], in0=ib_e[:], scalar1=1.0)
-            nc.scalar.activation(out=ib_e[:], in_=ib_e[:], func=ACTF.Ln)
-            nc.vector.scalar_tensor_tensor(out=bypass[:], in0=ib[:], scalar=0.0, in1=ib_e[:],
-                                           op0=ALU.max, op1=ALU.add)
-
-
         band_pool = ctx.enter_context(tc.tile_pool(name="band_pool", bufs=2))
         gain_pool = ctx.enter_context(tc.tile_pool(name="gain_pool", bufs=2))
         vf_pool = ctx.enter_context(tc.tile_pool(name="vf_pool", bufs=2))
@@ -179,9 +189,14 @@ def tile_dwarfattention_pa_t_kernel(tc, x, W_qkv, b_qkv, gains, pos_bias, identi
         rows_of_out = out.rearrange("b n e -> (b n) e")
         scratch = out.rearrange("b n e -> (b n e)")
 
-        def load_gains(b):
-            for h in range(H):
-                nc.sync.dma_start(out=g_raw[:, b, h, :, :], in_=gains[b, h].rearrange("(t p) j -> p t j", p=P))
+        def turn_gains():
+            for j0 in (0, G_BANK):
+                n = min(G_BANK, NS - j0)
+                g_tr = ps_tr.tile([P, G_BANK, P], BF16, name="g_tr", tag="tr")
+                for j in range(n):
+                    nc.tensor.transpose(out=g_tr[:, j, :], in_=g_rows[:, :, j0 + j], identity=ident_bf[:])
+                nc.vector.tensor_copy(out=g_raw[:].rearrange("p b h t j -> p (b h t) j")[:, :, j0:j0 + n],
+                                      in_=g_tr[:, 0:n, :].rearrange("p j r -> p r j"))
 
         def make_gain(c, tau):
             b, cc = divmod(c, NCC)
@@ -191,9 +206,9 @@ def tile_dwarfattention_pa_t_kernel(tc, x, W_qkv, b_qkv, gains, pos_bias, identi
                 nc.vector.memset(gain_of[c // GCH][:, :, TAP2 - 1:TAP2 + 1, :], 0.0)
                 nc.scalar.copy(out=gain_of[c // GCH][:, :, 0, :],
                                in_=bypass[:].unsqueeze(1).to_broadcast([P, n, H]))
-            for h in range(H):
-                nc.scalar.activation(out=gain_of[c // GCH][:, :, TAP_AT[tau]:TAP_AT[tau] + NS, h],
-                                     in_=g_raw[:, b, h, cc * TPC:cc * TPC + n, :], func=ACTF.Copy, scale=D4[tau])
+            nc.scalar.activation(out=gain_of[c // GCH][:, :, TAP_AT[tau]:TAP_AT[tau] + NS, :],
+                                 in_=g_raw[:, b, :, cc * TPC:cc * TPC + n, :].rearrange("p h t j -> p t j h"),
+                                 func=ACTF.Copy, scale=abs(D4[tau]))
 
         def transpose_x(c, tl):
             if tl == 0:
@@ -239,12 +254,8 @@ def tile_dwarfattention_pa_t_kernel(tc, x, W_qkv, b_qkv, gains, pos_bias, identi
             project(c, 0, qf_of[c][:])
 
         def project_v(c):
-            vf_of[c] = vf_pool.tile([P, VPAD + CH], F32, name="v_f")
-            if c % NCC == 0:
-                nc.vector.memset(vf_of[c][:, 0:VPAD], 0.0)
-            else:
-                nc.scalar.copy(out=vf_of[c][:, 0:VPAD], in_=vf_of[c - 1][:, CH:CH + VPAD])
-            project(c, 2, vf_of[c][:, VPAD:VPAD + CH])
+            vf_of[c] = vf_pool.tile([P, CH], F32, name="v_f")
+            project(c, 2, vf_of[c][:])
 
         def turn(src, first, tr):
             for tl in range(TPC):
@@ -291,9 +302,25 @@ def tile_dwarfattention_pa_t_kernel(tc, x, W_qkv, b_qkv, gains, pos_bias, identi
                         nc.sync.dma_start(out=keys[early:P, i, tl, :],
                                           in_=rows_of_out[row + tl * P + early:row + (tl + 1) * P, :])
 
-        def turn_v(c, shift, ring, size):
-            g0 = (c * TPC) % size
-            token_major(vf_of[c], VPAD - shift, ring[:, g0:g0 + TPC, :])
+        def turn_v(c):
+            g0 = (c * TPC) % VRING
+            token_major(vf_of[c], 0, v_tok[:, g0:g0 + TPC, :])
+            row = value_place(c) * CH
+            nc.sync.dma_start(out=rows_of_out[row:row + CH, :].rearrange("(t p) e -> p t e", p=P),
+                              in_=v_tok[:, g0:g0 + TPC, :])
+
+        def load_half(c):
+            g0 = (c * TPC) % BRING
+            row = value_place(c) * CH
+            if c % NCC == 0:
+                nc.vector.memset(v_half[0:SHIFT, g0, :], 0.0)
+            else:
+                last = (value_place(c - 1) + 1) * CH
+                nc.sync.dma_start(out=v_half[0:SHIFT, g0, :], in_=rows_of_out[last - SHIFT:last, :])
+            nc.sync.dma_start(out=v_half[SHIFT:P, g0, :], in_=rows_of_out[row:row + P - SHIFT, :])
+            first = row + P - SHIFT
+            nc.sync.dma_start(out=v_half[:, g0 + 1:g0 + TPC, :],
+                              in_=rows_of_out[first:first + (TPC - 1) * P, :].rearrange("(t p) e -> p t e", p=P))
 
         def whole_products(c, i):
             cc = c % NCC
@@ -385,10 +412,15 @@ def tile_dwarfattention_pa_t_kernel(tc, x, W_qkv, b_qkv, gains, pos_bias, identi
             u = tap_pool.tile([P, TPC, NTAP, H], F32, name="u")
             nc.vector.tensor_tensor(out=u[:, :, 0:TAP1, :], in0=score[:, :, 0:1, :].to_broadcast([P, TPC, TAP1, H]),
                                     in1=pb_bc[:, 0:TAP1, :].unsqueeze(1).to_broadcast([P, TPC, TAP1, H]), op=ALU.add)
-            for tap, place, ln in ((TAP1, 1, NPOW), (TAP2, 1, NPOW), (TAP3, 1 + NPOW, NTRI)):
-                nc.vector.tensor_tensor(out=u[:, :, tap:tap + ln, :], in0=score[:, :, place:place + ln, :],
-                                        in1=pb_bc[:, tap:tap + ln, :].unsqueeze(1).to_broadcast([P, TPC, ln, H]),
-                                        op=ALU.add)
+            twice = [P, TPC, 2, NPOW * H]
+            nc.vector.tensor_tensor(
+                out=u[:, :, TAP1:TAP3, :].rearrange("p t (a k) h -> p t a (k h)", a=2),
+                in0=score[:, :, 1:1 + NPOW, :].rearrange("p t k h -> p t (k h)").unsqueeze(2).to_broadcast(twice),
+                in1=pb_bc[:, TAP1:TAP3, :].rearrange("p (a k) h -> p a (k h)", a=2).unsqueeze(1)
+                .to_broadcast(twice), op=ALU.add)
+            nc.vector.tensor_tensor(out=u[:, :, TAP3:NTAP, :], in0=score[:, :, 1 + NPOW:NOFF, :],
+                                    in1=pb_bc[:, TAP3:NTAP, :].unsqueeze(1).to_broadcast([P, TPC, NTRI, H]),
+                                    op=ALU.add)
             f = tap_pool.tile([P, TPC, NTAP, H], F32, name="f")
             nc.scalar.activation(out=f[:], in_=u[:], func=ACTF.Exp)
             nc.scalar.activation(out=u[:], in_=u[:], func=ACTF.Relu)
@@ -405,13 +437,8 @@ def tile_dwarfattention_pa_t_kernel(tc, x, W_qkv, b_qkv, gains, pos_bias, identi
             nc.vector.tensor_tensor(out=w[:, :, 1:1 + NPOW, :], in0=w_tap[:, :, TAP1:TAP2, :],
                                     in1=w_tap[:, :, TAP2:TAP3, :], op=ALU.add)
             z = weight_pool.tile([P, TPC, H], F32, name="z")
-            z_tri = weight_pool.tile([P, TPC, H], F32, name="z_tri")
-            nc.vector.tensor_reduce(out=z[:], in_=w[:, :, 0:1 + NPOW, :].rearrange("p t s h -> p t h s"),
-                                    axis=AX.X, op=ALU.add)
-            nc.vector.tensor_reduce(out=z_tri[:], in_=w[:, :, 1 + NPOW:NOFF, :].rearrange("p t s h -> p t h s"),
-                                    axis=AX.X, op=ALU.add)
-            nc.vector.scalar_tensor_tensor(out=z[:], in0=z[:], scalar=1e-6, in1=z_tri[:], op0=ALU.add,
-                                           op1=ALU.subtract)
+            nc.vector.tensor_reduce(out=z[:], in_=w[:].rearrange("p t s h -> p t h s"), axis=AX.X, op=ALU.add)
+            nc.vector.tensor_scalar_add(out=z[:], in0=z[:], scalar1=1e-6)
             rz = weight_pool.tile([P, TPC, H], F32, name="rz")
             nc.vector.reciprocal(out=rz[:], in_=z[:])
             nc.vector.tensor_tensor(out=w[:], in0=w[:], in1=rz[:].unsqueeze(2).to_broadcast([P, TPC, NOFF, H]),
@@ -421,7 +448,8 @@ def tile_dwarfattention_pa_t_kernel(tc, x, W_qkv, b_qkv, gains, pos_bias, identi
         def skew(c):
             w = weight_of[c]
             for s in NEAR:
-                nc.scalar.copy(out=rows[:, :, :, P - OFFS[s]], in_=w[:, :, s, :].rearrange("p t h -> p h t"))
+                nc.scalar.activation(out=rows[:, :, :, P - OFFS[s]], in_=w[:, :, s, :].rearrange("p t h -> p h t"),
+                                     func=ACTF.Copy, scale=-1.0 if s > NPOW else 1.0)
             for h in range(H):
                 area = scratch[SCR0 + h * TPC * UNIT:SCR0 + (h + 1) * TPC * UNIT]
                 nc.scalar.dma_start(out=area.rearrange("(t p w) -> p t w", t=TPC, p=P), in_=rows[:, h, :, :])
@@ -469,23 +497,31 @@ def tile_dwarfattention_pa_t_kernel(tc, x, W_qkv, b_qkv, gains, pos_bias, identi
                         in1=weight_of[c][:, t:t + n, s, :].unsqueeze(3).to_broadcast([P, n, H, HD]), op=ALU.mult)
                 if not first:
                     nc.gpsimd.tensor_tensor(out=far[:, dead:TPC, :], in0=far[:, dead:TPC, :],
-                                            in1=part[:, dead:TPC, :], op=ALU.add)
+                                            in1=part[:, dead:TPC, :], op=ALU.subtract if s > NPOW else ALU.add)
 
         def last_far_values(c):
             far_of[c] = far_pool.tile([P, TPC, E], F32, name="far")
+            negative = weight_pool.tile([P, TPC, NTRI, H], F32, name="negative")
+            nc.scalar.activation(out=negative[:], in_=weight_of[c][:, :, 1 + NPOW:NOFF, :], func=ACTF.Copy, scale=-1.0)
             for s in FAR:
                 for tl in range(TPC):
                     g = c * TPC + tl
                     for h in range(H):
                         hs = slice(h * HD, (h + 1) * HD)
-                        weight = weight_of[c][:, tl, s, h:h + 1]
+                        if s > NPOW:
+                            weight = negative[:, tl, s - 1 - NPOW, h:h + 1]
+                        else:
+                            weight = weight_of[c][:, tl, s, h:h + 1]
+                        if OFFS[s] % P == 0:
+                            value = v_tok[:, (g - OFFS[s] // P) % VRING, hs]
+                        else:
+                            value = v_half[:, (g - 1) % BRING, hs]
                         if s == FAR[0]:
-                            nc.vector.tensor_scalar_mul(out=far_of[c][:, tl, hs], in0=v_half[:, (g - 1) % BRING, hs],
-                                                        scalar1=weight)
+                            nc.vector.tensor_scalar_mul(out=far_of[c][:, tl, hs], in0=value, scalar1=weight)
                         else:
                             nc.vector.scalar_tensor_tensor(
-                                out=far_of[c][:, tl, hs], in0=v_tok[:, (g - OFFS[s] // P) % VRING, hs],
-                                scalar=weight, in1=far_of[c][:, tl, hs], op0=ALU.mult, op1=ALU.add)
+                                out=far_of[c][:, tl, hs], in0=value, scalar=weight, in1=far_of[c][:, tl, hs],
+                                op0=ALU.mult, op1=ALU.add)
 
         def near_values(c, h, tl):
             cc = c % NCC
@@ -518,8 +554,8 @@ def tile_dwarfattention_pa_t_kernel(tc, x, W_qkv, b_qkv, gains, pos_bias, identi
                     load_x(c + 3)
                 if is_chunk(c + 1):
                     quantise_x(c + 1)
-            if slot == 8 and c + 1 in (0, NCC):
-                load_gains((c + 1) // NCC)
+            if slot == 8 and c + 1 == 0:
+                turn_gains()
             if slot % 4 == 1 and is_chunk(c + 2):
                 transpose_x(c + 2, slot // 4)
             if is_chunk(c + 1):
@@ -534,9 +570,9 @@ def tile_dwarfattention_pa_t_kernel(tc, x, W_qkv, b_qkv, gains, pos_bias, identi
                 if slot in (7, 9):
                     load_keys(c + 1, (slot - 7) // 2)
                 if slot == 8:
-                    turn_v(c + 1, 0, v_tok, VRING)
-                if slot == 10:
-                    turn_v(c + 1, VPAD, v_half, BRING)
+                    turn_v(c + 1)
+                if slot == 12:
+                    load_half(c + 1)
                 if slot == 13:
                     turn_q(c + 1)
             if is_chunk(c):

from contextlib import ExitStack

import concourse.mybir as mybir
from concourse.masks import make_identity

F32 = mybir.dt.float32
BF16 = mybir.dt.bfloat16
U32 = mybir.dt.uint32
U8 = mybir.dt.uint8
FP8X4 = mybir.dt.float8_e4m3fn_x4
ALU = mybir.AluOpType
ACTF = mybir.ActivationFunctionType
AX = mybir.AxisListType

P = 128
B, N, D, H, HD, NS = 2, 4096, 1024, 2, 64, 11
E = H * HD
CH = 512
TPC = CH // P
NCC = N // CH
NT = N // P
NCHUNK = B * NCC
D4 = (0.4829629131445341, 0.8365163037378079, 0.2241438680420134, -0.1294095225512604)
NPOW, NTRI = 12, 11
OFFS = (0,) + tuple(1 << i for i in range(NPOW)) + tuple(3 << j for j in range(NTRI))
NOFF = len(OFFS)
RISING = sorted(range(NOFF), key=lambda s: OFFS[s])
NEAR = [s for s in RISING if OFFS[s] <= P]
FAR = [s for s in range(NOFF) if OFFS[s] > P]
WHOLE = [s for s in range(NOFF) if OFFS[s] % P == 0]
CUT = [s for s in range(1, 1 + NPOW) if OFFS[s] % P != 0]
MOVED = [s for s in range(1 + NPOW, NOFF) if OFFS[s] % P != 0]
DENSE = MOVED + [OFFS.index(P)]
SPARSE = [s for s in WHOLE if s not in DENSE]
NFEW = 4
NG, NR = 8, 8
NCOL = len(DENSE) * H
KPAD = 64
TAP0, TAP1, TAP2, TAP3 = 1, 12, 24, 36
NTAP = 47
TAP_AT = (TAP0, TAP1, TAP2 + 1, TAP3)
SHIFT = 64
G_BANK = 8
GCH = 1
ROW = 2 * P + 8
UNIT = P * ROW
VRING = 36
BRING = 12
SCR0 = B * N * E - H * TPC * UNIT
HOLD0 = NCC - 2
KPLACES = 3
FLOPS = 2 * B * N * D * 3 * E + 4 * B * H * N * HD * NOFF


def dead_tiles(cc, s):
    first = max(0, -((P - 1 - OFFS[s]) // P))
    return min(TPC, max(0, first - cc * TPC))


def key_place(c):
    return c if c < HOLD0 else HOLD0 + (c - HOLD0) % KPLACES


def value_place(c):
    return HOLD0 + KPLACES + c % 2


def runs_of(places):
    runs = []
    for i, s in enumerate(places):
        if runs and runs[-1][1] + runs[-1][2] == s:
            runs[-1][2] += 1
        else:
            runs.append([i, s, 1])
    return runs


def tile_dwarfattention_pa_t_kernel(tc, x, W_qkv, b_qkv, gains, pos_bias, identity_bypass, out):
    nc = tc.nc
    with ExitStack() as ctx:
        const = ctx.enter_context(tc.tile_pool(name="const", bufs=1))
        ps_tr = ctx.enter_context(tc.psum_pool(name="ps_tr", bufs=2))
        ps_q = ctx.enter_context(tc.psum_pool(name="ps_q", bufs=1))
        ps_cut = ctx.enter_context(tc.psum_pool(name="ps_cut", bufs=2))
        ps_sum = ctx.enter_context(tc.psum_pool(name="ps_sum", bufs=2))
        ps_near = ctx.enter_context(tc.psum_pool(name="ps_near", bufs=1))

        ident = const.tile([P, P], F32, name="ident")
        make_identity(nc, ident[:])
        ident_bf = const.tile([P, P], BF16, name="ident_bf")
        make_identity(nc, ident_bf[:])
        w_codes = const.tile([P, 2, 3 * P], U32, name="w_codes", align_bytes=64)
        w_scales = const.tile([P, 2, 3 * P], U8, name="w_scales", align_bytes=64)
        bias_col = const.tile([P, 4], F32, name="bias_col")
        pb_bc = const.tile([P, NTAP, H], F32, name="pb_bc")
        g_raw = const.tile([P, B, H, NT, NS], BF16, name="g_raw")
        bypass = const.tile([P, H], F32, name="bypass")
        k_tok = const.tile([P, NT, E], F32, name="k_tok")
        v_tok = const.tile([P, VRING, E], F32, name="v_tok")
        v_half = const.tile([P, BRING, E], F32, name="v_half")
        held = const.tile([P, (NCHUNK - HOLD0) * TPC, E], F32, name="held")
        spare = const.tile([P, HD], F32, name="spare")
        rows = const.tile([P, H, TPC, ROW], F32, name="rows")
        g_rows = const.tile([P, P, NS], BF16, name="g_rows")
        nc.gpsimd.memset(rows[:], 0.0)
        nc.gpsimd.memset(pb_bc[:], 0.0)

        x_pool = ctx.enter_context(tc.tile_pool(name="x_pool", bufs=2))
        grouped_pool = ctx.enter_context(tc.tile_pool(name="grouped_pool", bufs=1))
        code_pool = ctx.enter_context(tc.tile_pool(name="code_pool", bufs=1))
        x_of = {}

        def load_x(c):
            b, cc = divmod(c, NCC)
            x_of[c] = x_pool.tile([P, TPC, D], BF16, name="x_sb")
            rows_of_x = x[b, cc * CH:(cc + 1) * CH, :].rearrange("(t p) k -> p t k", p=P)
            step = 1 if c == 0 else TPC
            for t in range(0, TPC, step):
                nc.sync.dma_start(out=x_of[c][:, t:t + step, :], in_=rows_of_x[:, t:t + step, :])

        with tc.manual_schedule(), tc.tile_pool(name="setup", bufs=1) as setup:
            ib_raw = setup.tile([P, H], BF16, name="ib_raw")
            nc.sync.dma_start(out=ib_raw[:], in_=identity_bypass.partition_broadcast(P))
            b_rows = setup.tile([P, P], BF16, name="b_rows")
            nc.vector.memset(b_rows[:], 0.0)
            nc.sync.dma_start(out=b_rows[0:3, :], in_=b_qkv.rearrange("(f c) -> f c", c=P))
            w_sb = setup.tile([P, 3, D], BF16, name="w_sb")
            nc.sync.dma_start(out=w_sb[:], in_=W_qkv.rearrange("(f p) k -> p f k", p=P))
            load_x(0)
            pb_raw = setup.tile([P, 4 * NS * H], BF16, name="pb_raw")
            nc.sync.dma_start(out=pb_raw[:], in_=pos_bias.rearrange("r h -> (r h)").partition_broadcast(P))
            load_x(1)
            nc.sync.dma_start(out=g_rows[:], in_=gains.rearrange("b h (t p) j -> (b h t) p j", p=P))

            ib = setup.tile([P, H], F32, name="ib")
            nc.vector.tensor_copy(out=ib[:], in_=ib_raw[:])
            ib_e = setup.tile([P, H], F32, name="ib_e")
            nc.scalar.activation(out=ib_e[:], in_=ib[:], func=ACTF.Abs)
            nc.scalar.activation(out=ib_e[:], in_=ib_e[:], func=ACTF.Exp, scale=-1.0)
            nc.vector.tensor_scalar_add(out=ib_e[:], in0=ib_e[:], scalar1=1.0)
            nc.scalar.activation(out=ib_e[:], in_=ib_e[:], func=ACTF.Ln)
            nc.vector.scalar_tensor_tensor(out=bypass[:], in0=ib[:], scalar=0.0, in1=ib_e[:],
                                           op0=ALU.max, op1=ALU.add)

            w_grouped = setup.tile([P, 2, 3 * P, 2], F32, name="w_grouped", align_bytes=64)
            for f in range(3):
                w_tr = ps_tr.tile([P, 4, P], F32, name="w_tr", tag="tr")
                words = w_sb[:, f, :].bitcast(F32)
                for g in range(2):
                    for u in range(2):
                        nc.tensor.transpose(out=w_tr[:, 2 * g + u, :],
                                            in_=words[:, 2 * P * g + u:2 * P * (g + 1):2], identity=ident[:])
                nc.vector.tensor_copy(out=w_grouped[:, :, f * P:(f + 1) * P, :],
                                      in_=w_tr[:].rearrange("p (g u) r -> p g r u", u=2))
            for g in range(2):
                for f in range(3):
                    nc.vector.quantize_mx(
                        out=w_codes[:, g, f * P:(f + 1) * P].bitcast(FP8X4),
                        scales=w_scales[:, g, f * P:(f + 1) * P],
                        in_=w_grouped[:, g, f * P:(f + 1) * P, :].rearrange("p r u -> p (r u)").bitcast(BF16))

            b_rows32 = setup.tile([P, P], F32, name="b_rows32")
            nc.vector.tensor_copy(out=b_rows32[:], in_=b_rows[:])
            b_tr = ps_tr.tile([P, 4, P], F32, name="b_tr", tag="tr")
            nc.tensor.transpose(out=b_tr[:, 0, :], in_=b_rows32[:], identity=ident[:])
            nc.vector.tensor_copy(out=bias_col[:, 0:3], in_=b_tr[:, 0, 0:3])

            pb_view = pb_raw[:].rearrange("p (j t h) -> p t j h", t=4, h=H)
            for tau in range(4):
                nc.vector.tensor_copy(out=pb_bc[:, TAP_AT[tau]:TAP_AT[tau] + NS, :], in_=pb_view[:, tau, :, :])

        band_pool = ctx.enter_context(tc.tile_pool(name="band_pool", bufs=2))
        gain_pool = ctx.enter_context(tc.tile_pool(name="gain_pool", bufs=2))
        vf_pool = ctx.enter_context(tc.tile_pool(name="vf_pool", bufs=2))
        q_pool = ctx.enter_context(tc.tile_pool(name="q_pool", bufs=2))
        whole_pool = ctx.enter_context(tc.tile_pool(name="whole_pool", bufs=1))
        key_pool = ctx.enter_context(tc.tile_pool(name="key_pool", bufs=3))
        cut_pool = ctx.enter_context(tc.tile_pool(name="cut_pool", bufs=3))
        prod_pool = ctx.enter_context(tc.tile_pool(name="prod_pool", bufs=3))
        sum_pool = ctx.enter_context(tc.tile_pool(name="sum_pool", bufs=2))
        score_pool = ctx.enter_context(tc.tile_pool(name="score_pool", bufs=3))
        tap_pool = ctx.enter_context(tc.tile_pool(name="tap_pool", bufs=2))
        weight_pool = ctx.enter_context(tc.tile_pool(name="weight_pool", bufs=3))
        far_pool = ctx.enter_context(tc.tile_pool(name="far_pool", bufs=2))
        out_pool = ctx.enter_context(tc.tile_pool(name="out_pool", bufs=2))

        key_of, sum_of, grouped_of, code_of, kf_of, qf_of, q_of, vf_of, whole_of, gain_of = [{} for i in range(10)]
        cut_of, q_ps_of, score_of, weight_of, skewed_of, band_of, far_of, near_of = {}, {}, {}, {}, {}, {}, {}, {}
        rows_of_out = out.rearrange("b n e -> (b n) e")
        scratch = out.rearrange("b n e -> (b n e)")

        def turn_gains():
            for j0 in (0, G_BANK):
                n = min(G_BANK, NS - j0)
                g_tr = ps_tr.tile([P, G_BANK, P], BF16, name="g_tr", tag="tr")
                for j in range(n):
                    nc.tensor.transpose(out=g_tr[:, j, :], in_=g_rows[:, :, j0 + j], identity=ident_bf[:])
                nc.vector.tensor_copy(out=g_raw[:].rearrange("p b h t j -> p (b h t) j")[:, :, j0:j0 + n],
                                      in_=g_tr[:, 0:n, :].rearrange("p j r -> p r j"))

        def make_gain(c, tau):
            b, cc = divmod(c, NCC)
            n = GCH * TPC
            if tau == 0:
                gain_of[c // GCH] = gain_pool.tile([P, n, NTAP, H], F32, name="gain")
                nc.vector.memset(gain_of[c // GCH][:, :, TAP2 - 1:TAP2 + 1, :], 0.0)
                nc.scalar.copy(out=gain_of[c // GCH][:, :, 0, :],
                               in_=bypass[:].unsqueeze(1).to_broadcast([P, n, H]))
            nc.scalar.activation(out=gain_of[c // GCH][:, :, TAP_AT[tau]:TAP_AT[tau] + NS, :],
                                 in_=g_raw[:, b, :, cc * TPC:cc * TPC + n, :].rearrange("p h t j -> p t j h"),
                                 func=ACTF.Copy, scale=abs(D4[tau]))

        def transpose_x(c, tl):
            if tl == 0:
                grouped_of[c] = grouped_pool.tile([P, 2, CH, 2], F32, name="grouped", align_bytes=64)
            x_tr = ps_tr.tile([P, 4, P], F32, name="x_tr", tag="tr")
            words = x_of[c][:, tl, :].bitcast(F32)
            for g in range(2):
                for u in range(2):
                    nc.tensor.transpose(out=x_tr[:, 2 * g + u, :],
                                        in_=words[:, 2 * P * g + u:2 * P * (g + 1):2], identity=ident[:])
            nc.scalar.copy(out=grouped_of[c][:, :, tl * P:(tl + 1) * P, :],
                           in_=x_tr[:].rearrange("p (g u) r -> p g r u", u=2))

        def quantise_x(c):
            codes = code_pool.tile([P, 2, CH], U32, name="codes", align_bytes=64)
            scales = code_pool.tile([P, 2, CH], U8, name="scales", align_bytes=64)
            for g in range(2):
                nc.vector.quantize_mx(
                    out=codes[:, g, :].bitcast(FP8X4), scales=scales[:, g, :],
                    in_=grouped_of[c][:, g, :, :].rearrange("p r u -> p (r u)").bitcast(BF16))
            code_of[c] = (codes, scales)

        def project(c, f, dst):
            codes, scales = code_of[c]
            acc = ps_tr.tile([P, CH], F32, name="acc", tag="tr")
            for g in range(2):
                nc.tensor.matmul_mx(out=acc[:], lhsT=w_codes[:, g, f * P:(f + 1) * P].bitcast(FP8X4),
                                    lhsT_scale=w_scales[:, g, f * P:(f + 1) * P],
                                    rhs=codes[:, g, :].bitcast(FP8X4), rhs_scale=scales[:, g, :],
                                    start=(g == 0), stop=(g == 1))
            nc.scalar.activation(out=dst, in_=acc[:], func=ACTF.Identity, bias=bias_col[:, f:f + 1], scale=1.0)

        def project_k(c):
            kf_of[c] = vf_pool.tile([P, KPAD + CH], F32, name="k_f")
            if c % NCC == 0:
                nc.vector.memset(kf_of[c][:, 0:KPAD], 0.0)
            else:
                nc.scalar.copy(out=kf_of[c][:, 0:KPAD], in_=kf_of[c - 1][:, CH:CH + KPAD])
            project(c, 1, kf_of[c][:, KPAD:KPAD + CH])

        def project_q(c):
            qf_of[c] = q_pool.tile([P, CH], F32, name="q_f")
            project(c, 0, qf_of[c][:])

        def project_v(c):
            vf_of[c] = vf_pool.tile([P, CH], F32, name="v_f")
            project(c, 2, vf_of[c][:])

        def turn(src, first, tr):
            for tl in range(TPC):
                nc.tensor.transpose(out=tr[:, tl, :], in_=src[:, first + tl * P:first + (tl + 1) * P],
                                    identity=ident[:])

        def token_major(src, first, dst):
            tr = ps_tr.tile([P, TPC, P], F32, name="tok_tr", tag="tr")
            turn(src, first, tr)
            nc.scalar.copy(out=dst, in_=tr[:])

        def turn_q(c):
            q_ps_of[c] = ps_q.tile([P, TPC, P], F32, name="q_ps")
            turn(qf_of[c], 0, q_ps_of[c])
            q_of[c] = q_pool.tile([P, TPC, E], F32, name="q_tok")
            nc.scalar.copy(out=q_of[c][:], in_=q_ps_of[c][:])

        def turn_k(c):
            t0 = (c % NCC) * TPC
            token_major(kf_of[c], KPAD, k_tok[:, t0:t0 + TPC, :])
            row = key_place(c) * CH
            nc.sync.dma_start(out=rows_of_out[row:row + CH, :].rearrange("(t p) e -> p t e", p=P),
                              in_=k_tok[:, t0:t0 + TPC, :])

        def load_keys(c, half):
            keys = key_pool.tile([P, len(MOVED), 2, E], F32, name="keys")
            key_of[(c, half)] = keys
            for i, s in enumerate(MOVED):
                o = OFFS[s]
                row = key_place(c) * CH + half * 2 * P - o
                joined = c % NCC != 0 and key_place(c) == key_place(c - 1) + 1
                if half == 1 or joined:
                    nc.sync.dma_start(out=keys[:, i, :, :],
                                      in_=rows_of_out[row:row + 2 * P, :].rearrange("(t p) e -> p t e", p=P))
                    continue
                for tl in range(2):
                    early = min(P, max(0, o - tl * P))
                    if early and c % NCC == 0:
                        nc.vector.memset(keys[0:early, i, tl, :], 0.0)
                    if early and c % NCC != 0:
                        last = key_place(c - 1) * CH + CH + tl * P - o
                        nc.sync.dma_start(out=keys[0:early, i, tl, :], in_=rows_of_out[last:last + early, :])
                    if early < P:
                        nc.sync.dma_start(out=keys[early:P, i, tl, :],
                                          in_=rows_of_out[row + tl * P + early:row + (tl + 1) * P, :])

        def turn_v(c):
            g0 = (c * TPC) % VRING
            token_major(vf_of[c], 0, v_tok[:, g0:g0 + TPC, :])
            row = value_place(c) * CH
            nc.sync.dma_start(out=rows_of_out[row:row + CH, :].rearrange("(t p) e -> p t e", p=P),
                              in_=v_tok[:, g0:g0 + TPC, :])

        def load_half(c):
            g0 = (c * TPC) % BRING
            row = value_place(c) * CH
            if c % NCC == 0:
                nc.vector.memset(v_half[0:SHIFT, g0, :], 0.0)
            else:
                last = (value_place(c - 1) + 1) * CH
                nc.sync.dma_start(out=v_half[0:SHIFT, g0, :], in_=rows_of_out[last - SHIFT:last, :])
            nc.sync.dma_start(out=v_half[SHIFT:P, g0, :], in_=rows_of_out[row:row + P - SHIFT, :])
            first = row + P - SHIFT
            nc.sync.dma_start(out=v_half[:, g0 + 1:g0 + TPC, :],
                              in_=rows_of_out[first:first + (TPC - 1) * P, :].rearrange("(t p) e -> p t e", p=P))

        def whole_products(c, i):
            cc = c % NCC
            dead = dead_tiles(cc, SPARSE[i])
            if dead < TPC:
                first = cc * TPC - OFFS[SPARSE[i]] // P
                nc.vector.tensor_tensor(out=whole_of[c][:, i, dead:TPC, :], in0=k_tok[:, first + dead:first + TPC, :],
                                        in1=q_ps_of[c][:, dead:TPC, :], op=ALU.mult)

        def few_sums(prods, score):
            for h in range(H):
                nc.scalar.activation(out=spare[:], in_=prods[:, h * HD:(h + 1) * HD], func=ACTF.Copy,
                                     accum_out=score[:, h:h + 1])

        def whole_sums(c):
            cc = c % NCC
            for t in range(TPC):
                few_sums(whole_of[c][:, 0, t, :], score_of[c][:, t, 0, :])
            for dead in range(TPC):
                for j, s, ln in runs_of([s for s in SPARSE if s >= NFEW and dead_tiles(cc, s) == dead]):
                    i = SPARSE.index(s)
                    nc.vector.tensor_reduce(
                        out=score_of[c][:, dead:TPC, s:s + ln, :].rearrange("p t s h -> p s t h"),
                        in_=whole_of[c][:, i:i + ln, dead:TPC, :].rearrange("p s t (h d) -> p s t h d", h=H),
                        axis=AX.X, op=ALU.add)

        def cut_products(c, tl, part):
            if part == 0:
                cut_of[(c, tl)] = cut_pool.tile([P, len(CUT), E], F32, name="cut_prod")
            i0 = 4 * part
            n = len(CUT[i0:i0 + 4])
            cut = ps_cut.tile([P, 4, P], F32, name="cut")
            for j in range(n):
                first = KPAD + tl * P - OFFS[CUT[i0 + j]]
                nc.tensor.transpose(out=cut[:, j, :], in_=kf_of[c][:, first:first + P], identity=ident[:])
            nc.vector.tensor_tensor(out=cut_of[(c, tl)][:, i0:i0 + n, :], in0=cut[:, 0:n, :],
                                    in1=q_of[c][:, tl, :].unsqueeze(1).to_broadcast([P, n, E]), op=ALU.mult)

        def cut_sums(c, tl):
            prod = cut_of[(c, tl)]
            i = CUT.index(NFEW)
            for j in range(i):
                few_sums(prod[:, j, :], score_of[c][:, tl, CUT[j], :])
            nc.vector.tensor_reduce(out=score_of[c][:, tl, NFEW:CUT[-1] + 1, :],
                                    in_=prod[:, i:len(CUT), :].rearrange("p s (h d) -> p s h d", h=H),
                                    axis=AX.X, op=ALU.add)

        def dense_products(c, tl):
            t = (c % NCC) * TPC + tl
            q_t = q_ps_of[c][:, tl, :]
            prod = prod_pool.tile([P, NG, NCOL, NR], F32, name="prod")

            def times_q(keys, i, n):
                nc.vector.tensor_tensor(
                    out=prod[:, :, i * H:(i + n) * H, :].rearrange("p g (s h) r -> p s h g r", h=H),
                    in0=keys.rearrange("p s (h g r) -> p s h g r", h=H, g=NG),
                    in1=q_t.rearrange("p (h g r) -> p h g r", h=H, g=NG).unsqueeze(1)
                    .to_broadcast([P, n, H, NG, NR]), op=ALU.mult)

            times_q(key_of[(c, tl // 2)][:, :, tl % 2, :], 0, len(MOVED))
            if t > 0:
                times_q(k_tok[:, t - 1:t, :], len(DENSE) - 1, 1)
            else:
                nc.vector.memset(prod[:, :, NCOL - H:NCOL, :], 0.0)
            bank = ps_sum.tile([P, CH], F32, name="bank")
            acc = bank[:, 0:P]
            for i in range(NG):
                nc.tensor.matmul(out=acc, lhsT=prod[:, i, :, :].rearrange("p k r -> p (k r)"), rhs=ident[:],
                                 is_transpose=True, start=(i == 0), stop=(i == NG - 1))
            nc.scalar.copy(out=sum_of[c][:, tl, :], in_=acc)

        def dense_scores(c):
            back = ps_tr.tile([P, TPC, P], F32, name="back", tag="tr")
            turn(sum_of[c][:].rearrange("p t k -> p (t k)"), 0, back)
            view = back[:].rearrange("p t (s h r) -> p t s h r", h=H, r=NR)
            for i, s, ln in runs_of(DENSE):
                nc.vector.tensor_reduce(out=score_of[c][:, :, s:s + ln, :], in_=view[:, :, i:i + ln, :, :],
                                        axis=AX.X, op=ALU.add)

        def open_scores(c):
            score_of[c] = score_pool.tile([P, TPC, NOFF, H], F32, name="score")
            whole_of[c] = whole_pool.tile([P, len(SPARSE), TPC, E], F32, name="whole")
            sum_of[c] = sum_pool.tile([P, TPC, P], F32, name="sum")
            if any(dead_tiles(c % NCC, s) for s in SPARSE):
                nc.vector.memset(score_of[c][:], 0.0)

        def weights(c):
            score = score_of[c]
            u = tap_pool.tile([P, TPC, NTAP, H], F32, name="u")
            nc.vector.tensor_tensor(out=u[:, :, 0:TAP1, :], in0=score[:, :, 0:1, :].to_broadcast([P, TPC, TAP1, H]),
                                    in1=pb_bc[:, 0:TAP1, :].unsqueeze(1).to_broadcast([P, TPC, TAP1, H]), op=ALU.add)
            twice = [P, TPC, 2, NPOW * H]
            nc.vector.tensor_tensor(
                out=u[:, :, TAP1:TAP3, :].rearrange("p t (a k) h -> p t a (k h)", a=2),
                in0=score[:, :, 1:1 + NPOW, :].rearrange("p t k h -> p t (k h)").unsqueeze(2).to_broadcast(twice),
                in1=pb_bc[:, TAP1:TAP3, :].rearrange("p (a k) h -> p a (k h)", a=2).unsqueeze(1)
                .to_broadcast(twice), op=ALU.add)
            nc.vector.tensor_tensor(out=u[:, :, TAP3:NTAP, :], in0=score[:, :, 1 + NPOW:NOFF, :],
                                    in1=pb_bc[:, TAP3:NTAP, :].unsqueeze(1).to_broadcast([P, TPC, NTRI, H]),
                                    op=ALU.add)
            f = tap_pool.tile([P, TPC, NTAP, H], F32, name="f")
            nc.scalar.activation(out=f[:], in_=u[:], func=ACTF.Exp)
            nc.scalar.activation(out=u[:], in_=u[:], func=ACTF.Relu)
            nc.vector.scalar_tensor_tensor(out=f[:], in0=f[:], scalar=1.0, in1=u[:], op0=ALU.min, op1=ALU.add)
            w_tap = tap_pool.tile([P, TPC, TAP3, H], F32, name="w_tap")
            w = weight_pool.tile([P, TPC, NOFF, H], F32, name="w")
            first = (c % GCH) * TPC
            g_c = gain_of[c // GCH][:, first:first + TPC, :, :]
            nc.vector.tensor_tensor(out=w_tap[:], in0=f[:, :, 0:TAP3, :], in1=g_c[:, :, 0:TAP3, :], op=ALU.mult)
            nc.vector.tensor_tensor(out=w[:, :, 1 + NPOW:NOFF, :], in0=f[:, :, TAP3:NTAP, :],
                                    in1=g_c[:, :, TAP3:NTAP, :], op=ALU.mult)
            nc.vector.tensor_reduce(out=w[:, :, 0, :], in_=w_tap[:, :, 0:TAP1, :].rearrange("p t k h -> p t h k"),
                                    axis=AX.X, op=ALU.add)
            nc.vector.tensor_tensor(out=w[:, :, 1:1 + NPOW, :], in0=w_tap[:, :, TAP1:TAP2, :],
                                    in1=w_tap[:, :, TAP2:TAP3, :], op=ALU.add)
            z = weight_pool.tile([P, TPC, H], F32, name="z")
            nc.vector.tensor_reduce(out=z[:], in_=w[:].rearrange("p t s h -> p t h s"), axis=AX.X, op=ALU.add)
            nc.vector.tensor_scalar_add(out=z[:], in0=z[:], scalar1=1e-6)
            rz = weight_pool.tile([P, TPC, H], F32, name="rz")
            nc.vector.reciprocal(out=rz[:], in_=z[:])
            nc.vector.tensor_tensor(out=w[:], in0=w[:], in1=rz[:].unsqueeze(2).to_broadcast([P, TPC, NOFF, H]),
                                    op=ALU.mult)
            weight_of[c] = w

        def skew(c):
            w = weight_of[c]
            for s in NEAR:
                nc.scalar.activation(out=rows[:, :, :, P - OFFS[s]], in_=w[:, :, s, :].rearrange("p t h -> p h t"),
                                     func=ACTF.Copy, scale=-1.0 if s > NPOW else 1.0)
            for h in range(H):
                area = scratch[SCR0 + h * TPC * UNIT:SCR0 + (h + 1) * TPC * UNIT]
                nc.scalar.dma_start(out=area.rearrange("(t p w) -> p t w", t=TPC, p=P), in_=rows[:, h, :, :])
                skewed_of[(c, h)] = band_pool.tile([P, TPC, 2 * P], F32, name="skewed")
                nc.sync.dma_start(out=skewed_of[(c, h)][:],
                                  in_=area.rearrange("(t r) -> t r", t=TPC)[:, 0:P * (ROW - 1)]
                                  .rearrange("t (p m) -> p t m", p=P)[:, :, 0:2 * P])

        def band(c, h, half):
            if half == 0:
                band_of[(c, h)] = band_pool.tile([P, 2 * TPC, P], F32, name="band")
            tr = ps_tr.tile([P, 4, P], F32, name="band_tr", tag="tr")
            for i in range(4):
                tl, kb = divmod(4 * half + i, 2)
                nc.tensor.transpose(out=tr[:, i, :], in_=skewed_of[(c, h)][:, tl, kb * P:(kb + 1) * P],
                                    identity=ident[:])
            nc.scalar.copy(out=band_of[(c, h)][:, 4 * half:4 * half + 4, :], in_=tr[:])

        def ring_pieces(first, n, size):
            at = first % size
            head = min(n, size - at)
            return [(0, at, head)] + ([(head, 0, n - head)] if head < n else [])

        def far_values(c):
            cc = c % NCC
            far_of[c] = far_pool.tile([P, TPC, E], F32, name="far")
            far = far_of[c]
            for s in FAR:
                dead = dead_tiles(cc, s)
                if dead == TPC:
                    continue
                first = s == FAR[0]
                if first and dead:
                    nc.gpsimd.memset(far[:, 0:dead, :], 0.0)
                part = far if first else far_pool.tile([P, TPC, E], F32, name="part")
                if OFFS[s] % P == 0:
                    ring, size, g = v_tok, VRING, c * TPC + dead - OFFS[s] // P
                else:
                    ring, size, g = v_half, BRING, c * TPC + dead - 1
                for i, at, n in ring_pieces(g, TPC - dead, size):
                    t = dead + i
                    nc.gpsimd.tensor_tensor(
                        out=part[:, t:t + n, :].rearrange("p t (h d) -> p t h d", h=H),
                        in0=ring[:, at:at + n, :].rearrange("p t (h d) -> p t h d", h=H),
                        in1=weight_of[c][:, t:t + n, s, :].unsqueeze(3).to_broadcast([P, n, H, HD]), op=ALU.mult)
                if not first:
                    nc.gpsimd.tensor_tensor(out=far[:, dead:TPC, :], in0=far[:, dead:TPC, :],
                                            in1=part[:, dead:TPC, :], op=ALU.subtract if s > NPOW else ALU.add)

        def last_far_values(c):
            far_of[c] = far_pool.tile([P, TPC, E], F32, name="far")
            negative = weight_pool.tile([P, TPC, NTRI, H], F32, name="negative")
            nc.scalar.activation(out=negative[:], in_=weight_of[c][:, :, 1 + NPOW:NOFF, :], func=ACTF.Copy, scale=-1.0)
            for s in FAR:
                for tl in range(TPC):
                    g = c * TPC + tl
                    for h in range(H):
                        hs = slice(h * HD, (h + 1) * HD)
                        if s > NPOW:
                            weight = negative[:, tl, s - 1 - NPOW, h:h + 1]
                        else:
                            weight = weight_of[c][:, tl, s, h:h + 1]
                        if OFFS[s] % P == 0:
                            value = v_tok[:, (g - OFFS[s] // P) % VRING, hs]
                        else:
                            value = v_half[:, (g - 1) % BRING, hs]
                        if s == FAR[0]:
                            nc.vector.tensor_scalar_mul(out=far_of[c][:, tl, hs], in0=value, scalar1=weight)
                        else:
                            nc.vector.scalar_tensor_tensor(
                                out=far_of[c][:, tl, hs], in0=value, scalar=weight, in1=far_of[c][:, tl, hs],
                                op0=ALU.mult, op1=ALU.add)

        def near_values(c, h, tl):
            cc = c % NCC
            hs = slice(h * HD, (h + 1) * HD)
            if h == 0 and tl == 0:
                near_of[c] = ps_near.tile([P, TPC, E], F32, name="near")
            blocks = [kb for kb in range(2) if cc * TPC + tl - 1 + kb >= 0]
            for kb in blocks:
                nc.tensor.matmul(out=near_of[c][:, tl, hs], lhsT=band_of[(c, h)][:, 2 * tl + kb, :],
                                 rhs=v_tok[:, (c * TPC + tl - 1 + kb) % VRING, hs],
                                 start=(kb == blocks[0]), stop=(kb == 1))

        def finish(c):
            b, cc = divmod(c, NCC)
            if c >= HOLD0:
                o_sb = held[:, (c - HOLD0) * TPC:(c - HOLD0 + 1) * TPC, :]
            else:
                o_tile = out_pool.tile([P, TPC, E], F32, name="o_tile")
                o_sb = o_tile[:]
            nc.vector.tensor_tensor(out=o_sb, in0=near_of[c][:], in1=far_of[c][:], op=ALU.add)
            if c < HOLD0:
                nc.sync.dma_start(out=out[b, cc * CH:(cc + 1) * CH, :].rearrange("(t p) e -> p t e", p=P), in_=o_sb)

        def is_chunk(c):
            return 0 <= c < NCHUNK

        def work(c, slot):
            if slot == 0:
                if is_chunk(c + 3) and c + 3 >= 2:
                    load_x(c + 3)
                if is_chunk(c + 1):
                    quantise_x(c + 1)
            if slot == 8 and c + 1 == 0:
                turn_gains()
            if slot % 4 == 1 and is_chunk(c + 2):
                transpose_x(c + 2, slot // 4)
            if is_chunk(c + 1):
                if slot == 2:
                    project_k(c + 1)
                if slot == 3:
                    project_q(c + 1)
                if slot == 4:
                    project_v(c + 1)
                if slot == 6:
                    turn_k(c + 1)
                if slot in (7, 9):
                    load_keys(c + 1, (slot - 7) // 2)
                if slot == 8:
                    turn_v(c + 1)
                if slot == 12:
                    load_half(c + 1)
                if slot == 13:
                    turn_q(c + 1)
            if is_chunk(c):
                if slot == 0:
                    open_scores(c)
                if slot < len(SPARSE):
                    whole_products(c, slot)
                if slot == len(SPARSE):
                    whole_sums(c)
                tl, part = divmod(slot, 4)
                if part == 0:
                    dense_products(c, tl)
                if part in (1, 2):
                    cut_products(c, tl, part - 1)
                if part == 3:
                    cut_sums(c, tl)
            if is_chunk(c) and c % GCH == 0 and slot % 4 == 3:
                make_gain(c, slot // 4)
            if is_chunk(c - 1):
                if slot == 2:
                    with tc.high_priority():
                        dense_scores(c - 1)
                        weights(c - 1)
                        skew(c - 1)
                    if c == NCHUNK:
                        last_far_values(c - 1)
                    else:
                        far_values(c - 1)
            if is_chunk(c - 2):
                if slot < 2 * H:
                    band(c - 2, slot // 2, slot % 2)
                if slot in (5, 9):
                    for tl in range(TPC):
                        near_values(c - 2, (slot - 5) // TPC, tl)
                if slot == 14:
                    finish(c - 2)

        for c in range(-2, NCHUNK):
            for slot in range(4 * TPC):
                work(c, slot)
        with tc.manual_schedule():
            for c in range(NCHUNK, NCHUNK + 2):
                for slot in range(4 * TPC):
                    work(c, slot)
        for c in range(HOLD0, NCHUNK):
            b, cc = divmod(c, NCC)
            nc.sync.dma_start(out=out[b, cc * CH:(cc + 1) * CH, :].rearrange("(t p) e -> p t e", p=P),
                              in_=held[:, (c - HOLD0) * TPC:(c - HOLD0 + 1) * TPC, :])
